import numpy as np
import ml_dtypes


def mxq(x, axis, fmt="e4m3"):
    dtype, down = {"e4m3": (ml_dtypes.float8_e4m3fn, 7), "e5m2": (ml_dtypes.float8_e5m2, 14)}[fmt]
    v = np.moveaxis(np.asarray(x, np.float32).astype(ml_dtypes.bfloat16).astype(np.float64), axis, -1)
    blocks = v.reshape(v.shape[:-1] + (-1, 32))
    amax = np.abs(blocks).max(-1, keepdims=True)
    byte = np.maximum(np.where(amax > 0, np.frexp(amax)[1] - 1 + 127, 0) - down, 1)
    scale = np.exp2(byte - 127.0)
    codes = (blocks / scale).astype(np.float32).astype(dtype).astype(np.float64)
    return np.moveaxis((codes * scale).reshape(v.shape), -1, axis)


WIDE = False


def mx_kscale(k):
    if not WIDE:
        return np.ones(k)
    levels = np.array([30, -30])
    if k % 512:
        return np.exp2(np.random.permutation(np.resize(levels, k // 32))).repeat(32)
    a = np.empty((k // 512, 16))
    for p in range(k // 512):
        a[p, :8] = np.random.permutation(np.resize(levels, 8))
        for g in range(8):
            far = levels[np.abs(levels - a[p, g]) >= 10]
            a[p, g + 8] = far[np.random.randint(len(far))]
    return np.exp2(a.ravel()).repeat(32)


BF16 = ml_dtypes.bfloat16


def bf(x):
    return np.asarray(x, np.float32).astype(BF16)


def f64(x):
    return np.asarray(x).astype(np.float64)


B, S, HID, NH, NG, HD, QB = 1, 1024, 1024, 16, 2, 128, 512
QSZ = NH * HD
KVSZ = NG * HD
QKV = QSZ + 2 * KVSZ
ROT = HD // 2
RP = ROT // 2


def rope(x, cache):
    b, nh, sq, hn = x.shape
    xr, x_pass = x[..., :ROT], x[..., ROT:]
    xs = xr.reshape(b, nh, sq, RP, 2)
    c = cache[:, :sq].reshape(-1, 1, sq, RP, 2)
    rot = np.stack([xs[..., 0] * c[..., 0] - xs[..., 1] * c[..., 1],
                    xs[..., 1] * c[..., 0] + xs[..., 0] * c[..., 1]], axis=-1)
    return np.concatenate([rot.reshape(b, nh, sq, ROT), x_pass], axis=-1)


def setup_inputs():
    s = mx_kscale(HID)
    return {"hidden_states": bf(np.random.standard_normal((B, S, HID)) * s),
            "rope_cache": bf(np.random.standard_normal((1, S, RP, 2))),
            "w_qkv": bf(np.random.standard_normal((HID, QKV)) / np.sqrt(HID) / s[:, None]),
            "b_qkv": bf(np.random.standard_normal(QKV) * 0.5)}


def reference(hidden_states, rope_cache, w_qkv, b_qkv):
    mixed = (mxq(f64(hidden_states), 2, "e5m2") @ mxq(f64(w_qkv), 0, "e4m3")) + f64(b_qkv)
    q = mixed[..., :QSZ].reshape(B, S, NH, HD).transpose(0, 2, 1, 3)
    k = mixed[..., QSZ:QSZ + KVSZ].reshape(B, S, NG, HD).transpose(0, 2, 1, 3)
    v = mixed[..., QSZ + KVSZ:].reshape(B, S, NG, HD).transpose(0, 2, 1, 3)
    c = f64(rope_cache)
    return rope(q, c), rope(k, c), v

@@ -1,0 +1,378 @@
+from contextlib import ExitStack
+
+import concourse.mybir as mybir
+from concourse.masks import make_identity
+
+S, HID, QKV = 1024, 1024, 2560
+FLOPS = 2 * S * HID * QKV
+
+F32 = mybir.dt.float32
+BF16 = mybir.dt.bfloat16
+U32 = mybir.dt.uint32
+U8 = mybir.dt.uint8
+E5M2 = mybir.dt.float8_e5m2_x4
+E4M3 = mybir.dt.float8_e4m3fn_x4
+ADD = mybir.AluOpType.add
+MULT = mybir.AluOpType.mult
+
+P = 128
+PACK = 4
+PASSES = 2
+CHUNK = 512
+CHUNKS = 5
+KV = 4
+HALF = 512
+HALVES = 2
+SUB = 4
+UNITS = CHUNKS * HALVES
+
+
+def tile_selfattention_pa_kernel(tc, hidden_states, rope_cache, w_qkv, b_qkv, out_0, out_1, out_2):
+    nc = tc.nc
+    with ExitStack() as ctx:
+        keep = ctx.enter_context(tc.tile_pool(name="keep", bufs=1))
+        stage = ctx.enter_context(tc.tile_pool(name="stage", bufs=2))
+        psum = ctx.enter_context(tc.psum_pool(name="psum", bufs=2))
+        ctx.enter_context(tc.manual_schedule())
+
+        def bank(tag, dtype=F32):
+            return psum.tile([P, 512 if dtype == F32 else 1024], dtype, name=tag, tag=tag)
+
+        ident_f32 = keep.tile([P, P], F32)
+        make_identity(nc, ident_f32[:])
+        ident_bf = keep.tile([P, P], BF16)
+        make_identity(nc, ident_bf[:])
+        sign = keep.tile([P, 1], F32)
+        nc.gpsimd.memset(sign[0:64, :], -1.0)
+        nc.gpsimd.memset(sign[64:128, :], 1.0)
+
+        bias_rows = keep.tile([P, CHUNK], BF16)
+        nc.vector.memset(bias_rows[:], 0.0)
+
+        cache = keep.tile([P, HALVES, SUB * 64], BF16)
+        nc.scalar.dma_start(out=cache[:], in_=rope_cache[0].rearrange("(a p s) j e -> p a (s j e)", a=HALVES, s=SUB))
+        nc.scalar.dma_start(out=bias_rows[0:CHUNKS, :], in_=b_qkv.rearrange("(c n) -> c n", n=CHUNK))
+
+        w_raw = keep.tile([P, CHUNKS, PASSES, PACK, CHUNK], BF16)
+        x_raw = keep.tile([P, HALVES, SUB, HID], BF16)
+        x_rows = hidden_states[0].rearrange("(a p s) k -> p a s k", a=HALVES, s=SUB)
+
+        def load_w(c, g):
+            rows = w_qkv[512 * g : 512 * (g + 1), CHUNK * c : CHUNK * (c + 1)]
+            nc.sync.dma_start(out=w_raw[:, c, g], in_=rows.rearrange("(p t) n -> p t n", t=PACK))
+
+        load_w(0, 0)
+        for s in range(SUB):
+            nc.sync.dma_start(out=x_raw[:, 0, s], in_=x_rows[:, 0, s])
+        load_w(0, 1)
+        for s in range(0, SUB, 2):
+            nc.sync.dma_start(out=x_raw[:, 1, s : s + 2], in_=x_rows[:, 1, s : s + 2])
+        for c in range(1, CHUNKS):
+            for g in range(PASSES):
+                load_w(c, g)
+
+        cache_rep = keep.tile([P, HALVES * SUB, 4, 32], F32)
+        cache_words = cache[:].rearrange("p a n -> p (a n)").bitcast(F32).rearrange("p (i j) -> p i j", j=32)
+        nc.vector.tensor_copy(out=cache_rep[:], in_=cache_words.unsqueeze(2).to_broadcast([P, HALVES * SUB, 4, 32]))
+        table = keep.tile([P, S], F32)
+        for a in range(HALVES):
+            t_ps = bank("even")
+            for s in range(SUB):
+                nc.tensor.transpose(
+                    t_ps[:, P * s : P * (s + 1)], cache_rep[:, SUB * a + s].rearrange("p r j -> p (r j)"), ident_f32[:]
+                )
+            nc.scalar.copy(out=table[:, HALF * a : HALF * (a + 1)], in_=t_ps[:])
+        table_pairs = table[:].bitcast(BF16).rearrange("p (n e) -> p n e", e=2)
+        c0 = table_pairs[:, :, 0]
+        c1 = table_pairs[:, :, 1]
+        neg_c1 = keep.tile([P, S], BF16)
+        signed_c1 = keep.tile([P, S], BF16)
+
+        x_group = keep.tile([P, HALVES, PASSES, HALF, 2], F32, align_bytes=64)
+        x_codes = keep.tile([P, HALVES, PASSES, HALF], U32, align_bytes=64)
+        x_scales = keep.tile([P, HALVES, PASSES, HALF], U8, align_bytes=64)
+
+        def transpose_x(a, s, tag):
+            words = x_raw[:, a, s].bitcast(F32)
+            x_ps = bank(tag)
+            for g in range(PASSES):
+                for u in range(2):
+                    i = 2 * g + u
+                    nc.tensor.transpose(
+                        x_ps[:, P * i : P * (i + 1)], words[:, 256 * g + u : 256 * (g + 1) : 2], ident_f32[:]
+                    )
+            nc.scalar.copy(
+                out=x_group[:, a, :, P * s : P * (s + 1), :],
+                in_=x_ps[:].rearrange("p (g u t) -> p g t u", g=PASSES, u=2),
+            )
+
+        def quantize_x(a, g):
+            nc.vector.quantize_mx(
+                out=x_codes[:, a, g].bitcast(E5M2),
+                scales=x_scales[:, a, g],
+                in_=x_group[:, a, g].rearrange("p t u -> p (t u)").bitcast(BF16),
+            )
+
+        rot_width = [256] * KV + [192]
+        pass_width = [256] * KV + [384]
+        widths = {"rot": rot_width, "pass": pass_width}
+        group = {}
+        codes = {}
+        scales = {}
+        for part in ("rot", "pass"):
+            for c in range(CHUNKS):
+                codes[part, c] = keep.tile([P, PASSES, widths[part][c]], U32, name="codes_%s%d" % (part, c), align_bytes=64)
+                scales[part, c] = keep.tile([P, PASSES, widths[part][c]], U8, name="scales_%s%d" % (part, c), align_bytes=64)
+
+        def interleave(part, c, g, copy):
+            if g == 0:
+                group[part, c] = stage.tile(
+                    [P, PASSES, widths[part][c], PACK], BF16, name="group_" + part, tag="group_" + part, align_bytes=64
+                )
+            dst = group[part, c][:, g]
+            raw = w_raw[:, c, g]
+            heads = 4 if c < KV else 2
+            if part == "rot":
+                src = raw.rearrange("p t (h r j e) -> p r e h j t", r=2, j=32, e=2)[:, 0, :, 0:heads]
+                n = heads * 32
+                copy(out=dst[:, 0 : 2 * n].rearrange("p (e h j) t -> p e h j t", e=2, j=32), in_=src)
+                if c == KV:
+                    copy(out=dst[:, 2 * n : 3 * n].rearrange("p (h j) t -> p h j t", j=32), in_=src[:, 0])
+            else:
+                src = raw.rearrange("p t (h r i) -> p r h i t", r=2, i=64)[:, 1, 0:heads]
+                n = heads * 64
+                copy(out=dst[:, 0:n].rearrange("p (h i) t -> p h i t", i=64), in_=src)
+                if c == KV:
+                    copy(out=dst[:, n : n + 256], in_=raw[:, :, 256:512].rearrange("p t n -> p n t"))
+
+        def quantize_w(part, c):
+            width = widths[part][c]
+            calls = 2 if width == 384 else 1
+            n = PASSES * width // calls
+            for i in range(calls):
+                nc.vector.quantize_mx(
+                    out=codes[part, c][:].rearrange("p g n -> p (g n)")[:, n * i : n * (i + 1)].bitcast(E4M3),
+                    scales=scales[part, c][:].rearrange("p g n -> p (g n)")[:, n * i : n * (i + 1)],
+                    in_=group[part, c][:].rearrange("p g n t -> p (g n t)")[:, PACK * n * i : PACK * n * (i + 1)],
+                )
+
+        bias_perm = keep.tile([P, 448], BF16)
+        bias = keep.tile([P, 1408 + 32], BF16)
+
+        def permute_bias():
+            pairs = bias_rows[:].rearrange("p (h r j e) -> p r e h j", r=2, j=32, e=2)[:, 0]
+            nc.vector.tensor_copy(out=bias_perm[:, 0:256].rearrange("p (e h j) -> p e h j", e=2, j=32), in_=pairs)
+            nc.vector.tensor_copy(
+                out=bias_perm[:, 256:384].rearrange("p (e h j) -> p e h j", e=2, j=32), in_=pairs[:, :, 0:2]
+            )
+            nc.vector.tensor_copy(out=bias_perm[:, 384:448].rearrange("p (h j) -> p h j", j=32), in_=pairs[:, 0, 0:2])
+
+        def spread_bias():
+            passing = bias_rows[:].rearrange("p (h r i) -> p r h i", r=2, i=64)[:, 1]
+            b_ps = bank("odd", BF16)
+            for c in range(KV):
+                nc.tensor.matmul(
+                    b_ps[:, 256 * c : 256 * (c + 1)].rearrange("p (h i) -> p h i", i=64),
+                    lhsT=ident_bf[:, c : c + 1].to_broadcast([P, P]),
+                    rhs=passing,
+                    start=True,
+                    stop=True,
+                )
+            b2_ps = bank("odd", BF16)
+            row = ident_bf[:, KV : KV + 1].to_broadcast([P, P])
+            nc.tensor.matmul(
+                b2_ps[:, 0:128].rearrange("p (h i) -> p h i", i=64), lhsT=row, rhs=passing[:, 0:2], start=True, stop=True
+            )
+            nc.tensor.matmul(b2_ps[:, 128:384], lhsT=row, rhs=bias_rows[:, 256:512], start=True, stop=True)
+            for i, m0 in enumerate((0, 128, 256, 320)):
+                nc.tensor.matmul(
+                    b2_ps[:, 384 + 8 * i : 384 + 8 * (i + 1)],
+                    lhsT=bias_perm[:, m0 : m0 + P],
+                    rhs=ident_bf[:, 0:8],
+                    start=True,
+                    stop=True,
+                )
+            nc.scalar.copy(out=bias[:, 1024:1440], in_=b2_ps[:, 0:416])
+            nc.scalar.copy(out=bias[:, 0:1024], in_=b_ps[:])
+
+        def bias_column(i, c):
+            n = 1408 + 8 * i + c
+            return bias[:, n : n + 1]
+
+        products = {}
+        results = {}
+        rotated = {}
+
+        def multiply_rot(u):
+            c, a = divmod(u, HALVES)
+            banks = []
+            for tag, m0 in (("even", 0), ("odd", 128 if c < KV else 64)):
+                acc = bank(tag)
+                for g in range(PASSES):
+                    nc.tensor.matmul_mx(
+                        out=acc[:],
+                        lhsT=codes["rot", c][:, g, m0 : m0 + P].bitcast(E4M3),
+                        lhsT_scale=scales["rot", c][:, g, m0 : m0 + P],
+                        rhs=x_codes[:, a, g].bitcast(E5M2),
+                        rhs_scale=x_scales[:, a, g],
+                        start=(g == 0),
+                        stop=(g == PASSES - 1),
+                    )
+                banks.append(acc)
+            tokens = slice(HALF * a, HALF * (a + 1))
+            if c < KV:
+                terms = [(0, 0, c0), (0, 0, c1), (1, 1, neg_c1), (1, 1, c0)]
+            else:
+                terms = [(0, 2, c0), (1, 3, signed_c1)]
+            products[u] = []
+            for i, (b, col, factor) in enumerate(terms):
+                prod = stage.tile([P, HALF], F32, name="prod%d" % i, tag="prod%d" % i, bufs=3)
+                nc.vector.scalar_tensor_tensor(
+                    out=prod[:], in0=banks[b][:], scalar=bias_column(col, c), in1=factor[:, tokens], op0=ADD, op1=MULT
+                )
+                products[u].append(prod)
+
+        def pass_banks(u):
+            c = u // HALVES
+            if c < KV:
+                return [("pass", (0, 1), 0, 256), ("pass", (2, 3), 0, 256)]
+            return [("rot", (0, 1, 2, 3), 0, 128), ("pass", (0, 1), 128, 256), ("pass", (2, 3), 128, 256)]
+
+        def multiply_pass(u, which):
+            c, a = divmod(u, HALVES)
+            tag, subs, n0, n = pass_banks(u)[which]
+            if which == 0:
+                results[u] = stage.tile([P, 4, SUB, P], F32, name="result", tag="result", bufs=4)
+            acc = bank(tag)
+            for i, s in enumerate(subs):
+                for g in range(PASSES):
+                    nc.tensor.matmul_mx(
+                        out=acc[:, n * i : n * (i + 1)],
+                        lhsT=x_codes[:, a, g, P * s : P * (s + 1)].bitcast(E5M2),
+                        lhsT_scale=x_scales[:, a, g, P * s : P * (s + 1)],
+                        rhs=codes["pass", c][:, g, n0 : n0 + n].bitcast(E4M3),
+                        rhs_scale=scales["pass", c][:, g, n0 : n0 + n],
+                        start=(g == 0),
+                        stop=(g == PASSES - 1),
+                    )
+            return acc
+
+        def add_bias(u, which, acc):
+            c = u // HALVES
+            tag, subs, n0, n = pass_banks(u)[which]
+            by_sub = results[u][:].rearrange("p h s d -> p s h d")[:, subs[0] : subs[-1] + 1]
+            if c < KV:
+                dst, heads = by_sub[:, :, :, 64:128], 4
+            elif which == 0:
+                dst, heads = by_sub[:, :, 0:2, 64:128], 2
+            else:
+                dst, heads = by_sub[:, :, 2:4, :], 2
+            b = bias[:, 256 * c + n0 : 256 * c + n0 + n].rearrange("p (h d) -> p h d", h=heads)
+            nc.vector.tensor_tensor(
+                out=dst,
+                in0=acc[:].rearrange("p (s h d) -> p s h d", s=len(subs), h=heads),
+                in1=b.unsqueeze(1).to_broadcast([P, len(subs), heads, n // heads]),
+                op=ADD,
+            )
+
+        def transpose_products(u):
+            c = u // HALVES
+            prods = products[u]
+            if c < KV:
+                sums = [(prods[0], prods[2]), (prods[3], prods[1])]
+            else:
+                sums = [(prods[0], prods[1])]
+            per_bank = SUB // len(sums)
+            rotated[u] = []
+            for s in range(SUB):
+                if s % per_bank == 0:
+                    r_ps = bank("rot")
+                    rotated[u].append(r_ps)
+                for e, terms in enumerate(sums):
+                    n0 = P * (len(sums) * (s % per_bank) + e)
+                    for i, prod in enumerate(terms):
+                        nc.tensor.matmul(
+                            r_ps[:, n0 : n0 + P],
+                            lhsT=prod[:, P * s : P * (s + 1)],
+                            rhs=ident_f32[:],
+                            start=(i == 0),
+                            stop=(i == 1),
+                            is_transpose=True,
+                        )
+
+        def copy_rotated(u):
+            c = u // HALVES
+            heads = 4 if c < KV else 2
+            per_bank = SUB // len(rotated[u])
+            by_sub = results[u][:].rearrange("p h s d -> p s h d")
+            for i, r_ps in enumerate(rotated[u]):
+                dst = by_sub[:, per_bank * i : per_bank * (i + 1), 0:heads, 0:64]
+                nc.scalar.copy(
+                    out=dst.rearrange("p s h (j e) -> p s h j e", e=2),
+                    in_=r_ps[:].rearrange("p (s e h j) -> p s h j e", s=per_bank, e=2, j=32),
+                )
+
+        def store(u):
+            c, a = divmod(u, HALVES)
+            tokens = slice(HALF * a, HALF * (a + 1))
+            src = results[u][:].rearrange("p h s d -> p h (s d)")
+            if c < KV:
+                parts = [(out_0[0, 4 * c : 4 * (c + 1), tokens, :], src)]
+            else:
+                parts = [(out_2[0, :, tokens, :], src[:, 2:4]), (out_1[0, :, tokens, :], src[:, 0:2])]
+            for dst, part in parts:
+                nc.sync.dma_start(out=dst.rearrange("h (p s) d -> p h (s d)", s=SUB), in_=part)
+
+        permute_bias()
+        interleave("rot", 0, 0, nc.vector.tensor_copy)
+        interleave("pass", 0, 0, nc.vector.tensor_copy)
+        nc.vector.tensor_scalar(out=neg_c1[:], in0=c1, scalar1=-1.0, scalar2=None, op0=MULT)
+        for s, tag in enumerate(("rot", "rot", "pass", "pass")):
+            transpose_x(0, s, tag)
+        spread_bias()
+        interleave("rot", 0, 1, nc.vector.tensor_copy)
+        interleave("pass", 0, 1, nc.scalar.copy)
+        quantize_x(0, 0)
+        quantize_w("rot", 0)
+        quantize_x(0, 1)
+        quantize_w("pass", 0)
+
+        multiply_rot(0)
+        transpose_x(1, 0, "rot")
+        transpose_x(1, 1, "rot")
+        acc_first = multiply_pass(0, 0)
+        transpose_x(1, 2, "even")
+        transpose_x(1, 3, "odd")
+        acc_second = multiply_pass(0, 1)
+        add_bias(0, 0, acc_first)
+        quantize_x(1, 0)
+        quantize_x(1, 1)
+        add_bias(0, 1, acc_second)
+        transpose_products(0)
+        interleave("rot", 1, 0, nc.scalar.copy)
+        interleave("rot", 1, 1, nc.scalar.copy)
+        multiply_rot(1)
+        quantize_w("rot", 1)
+
+        for u in range(1, UNITS):
+            c = u // HALVES
+            part = "rot" if u % HALVES == 0 else "pass"
+            ahead = c + 1 < CHUNKS
+            if ahead:
+                interleave(part, c + 1, 0, nc.scalar.copy)
+            copy_rotated(u - 1)
+            if ahead:
+                interleave(part, c + 1, 1, nc.scalar.copy)
+            store(u - 1)
+            accs = [multiply_pass(u, i) for i in range(len(pass_banks(u)))]
+            for i, acc in enumerate(accs):
+                add_bias(u, i, acc)
+            if ahead:
+                quantize_w(part, c + 1)
+            if u == UNITS - 4:
+                nc.vector.tensor_scalar(out=signed_c1[:], in0=c1, scalar1=sign[:], scalar2=None, op0=MULT)
+            if u + 1 < UNITS:
+                multiply_rot(u + 1)
+            transpose_products(u)
+        copy_rotated(UNITS - 1)
+        store(UNITS - 1)

@@ -24,7 +24,8 @@ KV = 4
 HALF = 512
 HALVES = 2
 SUB = 4
-UNITS = CHUNKS * HALVES
+UNITS = KV * HALVES
+VECTOR_COLUMNS = 384
 
 
 def tile_selfattention_pa_kernel(tc, hidden_states, rope_cache, w_qkv, b_qkv, out_0, out_1, out_2):
@@ -42,10 +43,6 @@ def tile_selfattention_pa_kernel(tc, hidden_states, rope_cache, w_qkv, b_qkv, ou
         make_identity(nc, ident_f32[:])
         ident_bf = keep.tile([P, P], BF16)
         make_identity(nc, ident_bf[:])
-        sign = keep.tile([P, 1], F32)
-        nc.gpsimd.memset(sign[0:64, :], -1.0)
-        nc.gpsimd.memset(sign[64:128, :], 1.0)
-
         bias_rows = keep.tile([P, CHUNK], BF16)
         nc.vector.memset(bias_rows[:], 0.0)
 
@@ -61,13 +58,16 @@ def tile_selfattention_pa_kernel(tc, hidden_states, rope_cache, w_qkv, b_qkv, ou
             rows = w_qkv[512 * g : 512 * (g + 1), CHUNK * c : CHUNK * (c + 1)]
             nc.sync.dma_start(out=w_raw[:, c, g], in_=rows.rearrange("(p t) n -> p t n", t=PACK))
 
-        load_w(0, 0)
+        def load_x(a, s0, s1):
+            nc.sync.dma_start(out=x_raw[:, a, s0:s1], in_=x_rows[:, a, s0:s1])
+
         for s in range(SUB):
-            nc.sync.dma_start(out=x_raw[:, 0, s], in_=x_rows[:, 0, s])
-        load_w(0, 1)
-        for s in range(0, SUB, 2):
-            nc.sync.dma_start(out=x_raw[:, 1, s : s + 2], in_=x_rows[:, 1, s : s + 2])
-        for c in range(1, CHUNKS):
+            load_x(0, s, s + 1)
+        load_w(KV, 0)
+        load_x(1, 0, 2)
+        load_x(1, 2, 4)
+        load_w(KV, 1)
+        for c in range(KV):
             for g in range(PASSES):
                 load_w(c, g)
 
@@ -81,12 +81,20 @@ def tile_selfattention_pa_kernel(tc, hidden_states, rope_cache, w_qkv, b_qkv, ou
                 nc.tensor.transpose(
                     t_ps[:, P * s : P * (s + 1)], cache_rep[:, SUB * a + s].rearrange("p r j -> p (r j)"), ident_f32[:]
                 )
-            nc.scalar.copy(out=table[:, HALF * a : HALF * (a + 1)], in_=t_ps[:])
+            nc.vector.tensor_copy(out=table[:, HALF * a : HALF * (a + 1)], in_=t_ps[:])
         table_pairs = table[:].bitcast(BF16).rearrange("p (n e) -> p n e", e=2)
         c0 = table_pairs[:, :, 0]
         c1 = table_pairs[:, :, 1]
         neg_c1 = keep.tile([P, S], BF16)
-        signed_c1 = keep.tile([P, S], BF16)
+
+        token_table = keep.tile([P, HALVES * SUB * 32, 2, 2], BF16)
+
+        def build_token_table():
+            pairs = cache[:].rearrange("p a (n e) -> p (a n) e", e=2)
+            nc.vector.tensor_copy(out=token_table[:, :, 0, 0], in_=pairs[:, :, 0])
+            nc.vector.tensor_scalar(out=token_table[:, :, 0, 1], in0=pairs[:, :, 1], scalar1=-1.0, scalar2=None, op0=MULT)
+            nc.vector.tensor_copy(out=token_table[:, :, 1, 0], in_=pairs[:, :, 1])
+            nc.vector.tensor_copy(out=token_table[:, :, 1, 1], in_=pairs[:, :, 0])
 
         x_group = keep.tile([P, HALVES, PASSES, HALF, 2], F32, align_bytes=64)
         x_codes = keep.tile([P, HALVES, PASSES, HALF], U32, align_bytes=64)
@@ -106,190 +114,225 @@ def tile_selfattention_pa_kernel(tc, hidden_states, rope_cache, w_qkv, b_qkv, ou
                 in_=x_ps[:].rearrange("p (g u t) -> p g t u", g=PASSES, u=2),
             )
 
-        def quantize_x(a, g):
+        def quantize_x(a, g0, g1):
             nc.vector.quantize_mx(
-                out=x_codes[:, a, g].bitcast(E5M2),
-                scales=x_scales[:, a, g],
-                in_=x_group[:, a, g].rearrange("p t u -> p (t u)").bitcast(BF16),
+                out=x_codes[:, a, g0:g1].rearrange("p g n -> p (g n)").bitcast(E5M2),
+                scales=x_scales[:, a, g0:g1].rearrange("p g n -> p (g n)"),
+                in_=x_group[:, a, g0:g1].rearrange("p g t u -> p (g t u)").bitcast(BF16),
             )
 
-        rot_width = [256] * KV + [192]
-        pass_width = [256] * KV + [384]
-        widths = {"rot": rot_width, "pass": pass_width}
         group = {}
         codes = {}
         scales = {}
-        for part in ("rot", "pass"):
-            for c in range(CHUNKS):
-                codes[part, c] = keep.tile([P, PASSES, widths[part][c]], U32, name="codes_%s%d" % (part, c), align_bytes=64)
-                scales[part, c] = keep.tile([P, PASSES, widths[part][c]], U8, name="scales_%s%d" % (part, c), align_bytes=64)
+        for name, width in [("kv", CHUNK)] + [((part, c), 256) for c in range(KV) for part in ("rot", "pass")]:
+            label = name if name == "kv" else "%s%d" % name
+            codes[name] = keep.tile([P, PASSES, width], U32, name="codes_" + label, align_bytes=64)
+            scales[name] = keep.tile([P, PASSES, width], U8, name="scales_" + label, align_bytes=64)
+        group["kv"] = keep.tile([P, PASSES, CHUNK, PACK], BF16, name="group_kv", align_bytes=64)
 
-        def interleave(part, c, g, copy):
+        def interleave_kv(g, copy, n0, n1):
+            copy(
+                out=group["kv"][:, g, n0:n1].rearrange("p (b i) t -> p b t i", i=4),
+                in_=w_raw[:, KV, g, :, n0:n1].rearrange("p t (b i) -> p b t i", i=4),
+            )
+
+        def interleave(part, c, g, copy=nc.scalar.copy):
             if g == 0:
                 group[part, c] = stage.tile(
-                    [P, PASSES, widths[part][c], PACK], BF16, name="group_" + part, tag="group_" + part, align_bytes=64
+                    [P, PASSES, 256, PACK], BF16, name="group_" + part, tag="group_" + part, bufs=3, align_bytes=64
                 )
             dst = group[part, c][:, g]
             raw = w_raw[:, c, g]
-            heads = 4 if c < KV else 2
             if part == "rot":
-                src = raw.rearrange("p t (h r j e) -> p r e h j t", r=2, j=32, e=2)[:, 0, :, 0:heads]
-                n = heads * 32
-                copy(out=dst[:, 0 : 2 * n].rearrange("p (e h j) t -> p e h j t", e=2, j=32), in_=src)
-                if c == KV:
-                    copy(out=dst[:, 2 * n : 3 * n].rearrange("p (h j) t -> p h j t", j=32), in_=src[:, 0])
+                src = raw.rearrange("p t (h r b i e) -> p r e h b t i", r=2, b=8, i=4, e=2)[:, 0]
+                for e in range(2):
+                    copy(out=dst[:, P * e : P * (e + 1)].rearrange("p (h b i) t -> p h b t i", b=8, i=4), in_=src[:, e])
             else:
-                src = raw.rearrange("p t (h r i) -> p r h i t", r=2, i=64)[:, 1, 0:heads]
-                n = heads * 64
-                copy(out=dst[:, 0:n].rearrange("p (h i) t -> p h i t", i=64), in_=src)
-                if c == KV:
-                    copy(out=dst[:, n : n + 256], in_=raw[:, :, 256:512].rearrange("p t n -> p n t"))
+                src = raw.rearrange("p t (h r b i) -> p r h b t i", r=2, b=16, i=4)[:, 1]
+                copy(out=dst.rearrange("p (h b i) t -> p h b t i", b=16, i=4), in_=src)
 
-        def quantize_w(part, c):
-            width = widths[part][c]
-            calls = 2 if width == 384 else 1
-            n = PASSES * width // calls
-            for i in range(calls):
-                nc.vector.quantize_mx(
-                    out=codes[part, c][:].rearrange("p g n -> p (g n)")[:, n * i : n * (i + 1)].bitcast(E4M3),
-                    scales=scales[part, c][:].rearrange("p g n -> p (g n)")[:, n * i : n * (i + 1)],
-                    in_=group[part, c][:].rearrange("p g n t -> p (g n t)")[:, PACK * n * i : PACK * n * (i + 1)],
-                )
+        def quantize_w(name, g0=0, g1=PASSES):
+            nc.vector.quantize_mx(
+                out=codes[name][:, g0:g1].rearrange("p g n -> p (g n)").bitcast(E4M3),
+                scales=scales[name][:, g0:g1].rearrange("p g n -> p (g n)"),
+                in_=group[name][:, g0:g1].rearrange("p g n t -> p (g n t)"),
+            )
 
-        bias_perm = keep.tile([P, 448], BF16)
-        bias = keep.tile([P, 1408 + 32], BF16)
+        bias_perm = keep.tile([P, 2, 4, 32], BF16)
+        bias = keep.tile([P, 1024 + CHUNK + 16], BF16)
 
         def permute_bias():
             pairs = bias_rows[:].rearrange("p (h r j e) -> p r e h j", r=2, j=32, e=2)[:, 0]
-            nc.vector.tensor_copy(out=bias_perm[:, 0:256].rearrange("p (e h j) -> p e h j", e=2, j=32), in_=pairs)
-            nc.vector.tensor_copy(
-                out=bias_perm[:, 256:384].rearrange("p (e h j) -> p e h j", e=2, j=32), in_=pairs[:, :, 0:2]
-            )
-            nc.vector.tensor_copy(out=bias_perm[:, 384:448].rearrange("p (h j) -> p h j", j=32), in_=pairs[:, 0, 0:2])
+            nc.vector.tensor_copy(out=bias_perm[:], in_=pairs)
 
         def spread_bias():
             passing = bias_rows[:].rearrange("p (h r i) -> p r h i", r=2, i=64)[:, 1]
-            b_ps = bank("odd", BF16)
+            kv_ps = bank("odd", BF16)
+            nc.tensor.matmul(
+                kv_ps[:, 0:CHUNK],
+                lhsT=ident_bf[:, KV : KV + 1].to_broadcast([P, P]),
+                rhs=bias_rows[:],
+                start=True,
+                stop=True,
+            )
+            for e in range(2):
+                nc.tensor.matmul(
+                    kv_ps[:, CHUNK + 8 * e : CHUNK + 8 * (e + 1)],
+                    lhsT=bias_perm[:, e].rearrange("p h j -> p (h j)"),
+                    rhs=ident_bf[:, 0:8],
+                    start=True,
+                    stop=True,
+                )
+            q_ps = bank("odd", BF16)
             for c in range(KV):
                 nc.tensor.matmul(
-                    b_ps[:, 256 * c : 256 * (c + 1)].rearrange("p (h i) -> p h i", i=64),
+                    q_ps[:, 256 * c : 256 * (c + 1)].rearrange("p (h i) -> p h i", i=64),
                     lhsT=ident_bf[:, c : c + 1].to_broadcast([P, P]),
                     rhs=passing,
                     start=True,
                     stop=True,
                 )
-            b2_ps = bank("odd", BF16)
-            row = ident_bf[:, KV : KV + 1].to_broadcast([P, P])
-            nc.tensor.matmul(
-                b2_ps[:, 0:128].rearrange("p (h i) -> p h i", i=64), lhsT=row, rhs=passing[:, 0:2], start=True, stop=True
+            return kv_ps, q_ps
+
+        def multiply_tokens(name, n0, a, pair, tag):
+            acc = bank(tag)
+            for i in range(2):
+                tokens = slice(P * (2 * pair + i), P * (2 * pair + i + 1))
+                for g in range(PASSES):
+                    nc.tensor.matmul_mx(
+                        out=acc[:, 256 * i : 256 * (i + 1)],
+                        lhsT=x_codes[:, a, g, tokens].bitcast(E5M2),
+                        lhsT_scale=x_scales[:, a, g, tokens],
+                        rhs=codes[name][:, g, n0 : n0 + 256].bitcast(E4M3),
+                        rhs_scale=scales[name][:, g, n0 : n0 + 256],
+                        start=(g == 0),
+                        stop=(g == PASSES - 1),
+                    )
+            return acc
+
+        def add_bias(dst, acc, b):
+            nc.vector.tensor_tensor(out=dst, in0=acc, in1=b.unsqueeze(1).to_broadcast(dst.shape), op=ADD)
+
+        def store(result, dst, a, s0=0, s1=SUB):
+            rows = dst[:, HALF * a : HALF * (a + 1), :].rearrange("h (p s) d -> p h s d", s=SUB)
+            nc.sync.dma_start(out=rows[:, :, s0:s1], in_=result[:, :, s0:s1])
+
+        keys = keep.tile([P, HALVES, 2, SUB, P], F32)
+        values = keep.tile([P, HALVES, 2, SUB, P], F32)
+        unrotated = keep.tile([P, HALVES, SUB, 2, 64], F32)
+        key_bias = bias[:, 1024:1280].rearrange("p (h d) -> p h d", h=2)
+        value_bias = bias[:, 1280:1536].rearrange("p (h d) -> p h d", h=2)
+
+        kv_banks = {}
+
+        def multiply_kv(a, s, g, tag=None):
+            if g == 0:
+                kv_banks[a, s] = bank(tag)
+            tokens = slice(P * s, P * (s + 1))
+            nc.tensor.matmul_mx(
+                out=kv_banks[a, s][:],
+                lhsT=x_codes[:, a, g, tokens].bitcast(E5M2),
+                lhsT_scale=x_scales[:, a, g, tokens],
+                rhs=codes["kv"][:, g].bitcast(E4M3),
+                rhs_scale=scales["kv"][:, g],
+                start=(g == 0),
+                stop=(g == PASSES - 1),
             )
-            nc.tensor.matmul(b2_ps[:, 128:384], lhsT=row, rhs=bias_rows[:, 256:512], start=True, stop=True)
-            for i, m0 in enumerate((0, 128, 256, 320)):
-                nc.tensor.matmul(
-                    b2_ps[:, 384 + 8 * i : 384 + 8 * (i + 1)],
-                    lhsT=bias_perm[:, m0 : m0 + P],
-                    rhs=ident_bf[:, 0:8],
-                    start=True,
-                    stop=True,
-                )
-            nc.scalar.copy(out=bias[:, 1024:1440], in_=b2_ps[:, 0:416])
-            nc.scalar.copy(out=bias[:, 0:1024], in_=b_ps[:])
 
-        def bias_column(i, c):
-            n = 1408 + 8 * i + c
-            return bias[:, n : n + 1]
+        def add_kv_bias(a, s):
+            acc = kv_banks[a, s][:].rearrange("p (h d) -> p h d", h=4)
+            nc.vector.tensor_tensor(out=unrotated[:, a, s], in0=acc[:, 0:2, 0:64], in1=key_bias[:, :, 0:64], op=ADD)
+            nc.vector.tensor_tensor(
+                out=keys[:, a, :, s, 64:128], in0=acc[:, 0:2, 64:128], in1=key_bias[:, :, 64:128], op=ADD
+            )
+            nc.vector.tensor_tensor(out=values[:, a, :, s], in0=acc[:, 2:4], in1=value_bias, op=ADD)
 
+        def rotate_keys(a, pair):
+            subs = slice(2 * pair, 2 * pair + 2)
+            shape = [P, 2, 2, 32, 2, 2]
+            terms = stage.tile(shape, F32, name="terms", tag="terms")
+            factors = token_table[:].rearrange("p (a s j) y e -> p a s j y e", a=HALVES, j=32)[:, a, subs]
+            nc.gpsimd.tensor_tensor(
+                out=terms[:],
+                in0=unrotated[:, a, subs].rearrange("p s h (j e) -> p s h j e", e=2).unsqueeze(4).to_broadcast(shape),
+                in1=factors.unsqueeze(2).to_broadcast(shape),
+                op=MULT,
+            )
+            by_term = terms[:].rearrange("p s h j y e -> p s h (j y) e")
+            nc.gpsimd.tensor_tensor(
+                out=keys[:, a].rearrange("p h s d -> p s h d")[:, subs, :, 0:64],
+                in0=by_term[:, :, :, :, 0],
+                in1=by_term[:, :, :, :, 1],
+                op=ADD,
+            )
+
+        rot_banks = {}
         products = {}
         results = {}
         rotated = {}
 
         def multiply_rot(u):
             c, a = divmod(u, HALVES)
-            banks = []
-            for tag, m0 in (("even", 0), ("odd", 128 if c < KV else 64)):
+            rot_banks[u] = []
+            products[u] = []
+            for e, tag in enumerate(("even", "odd")):
                 acc = bank(tag)
                 for g in range(PASSES):
                     nc.tensor.matmul_mx(
                         out=acc[:],
-                        lhsT=codes["rot", c][:, g, m0 : m0 + P].bitcast(E4M3),
-                        lhsT_scale=scales["rot", c][:, g, m0 : m0 + P],
+                        lhsT=codes["rot", c][:, g, P * e : P * (e + 1)].bitcast(E4M3),
+                        lhsT_scale=scales["rot", c][:, g, P * e : P * (e + 1)],
                         rhs=x_codes[:, a, g].bitcast(E5M2),
                         rhs_scale=x_scales[:, a, g],
                         start=(g == 0),
                         stop=(g == PASSES - 1),
                     )
-                banks.append(acc)
-            tokens = slice(HALF * a, HALF * (a + 1))
-            if c < KV:
-                terms = [(0, 0, c0), (0, 0, c1), (1, 1, neg_c1), (1, 1, c0)]
-            else:
-                terms = [(0, 2, c0), (1, 3, signed_c1)]
-            products[u] = []
-            for i, (b, col, factor) in enumerate(terms):
-                prod = stage.tile([P, HALF], F32, name="prod%d" % i, tag="prod%d" % i, bufs=3)
-                nc.vector.scalar_tensor_tensor(
-                    out=prod[:], in0=banks[b][:], scalar=bias_column(col, c), in1=factor[:, tokens], op0=ADD, op1=MULT
-                )
-                products[u].append(prod)
+                rot_banks[u].append(acc)
 
-        def pass_banks(u):
-            c = u // HALVES
-            if c < KV:
-                return [("pass", (0, 1), 0, 256), ("pass", (2, 3), 0, 256)]
-            return [("rot", (0, 1, 2, 3), 0, 128), ("pass", (0, 1), 128, 256), ("pass", (2, 3), 128, 256)]
-
-        def multiply_pass(u, which):
+        def form_products(u, first, last, n0=0, n1=HALF):
             c, a = divmod(u, HALVES)
-            tag, subs, n0, n = pass_banks(u)[which]
-            if which == 0:
-                results[u] = stage.tile([P, 4, SUB, P], F32, name="result", tag="result", bufs=4)
-            acc = bank(tag)
-            for i, s in enumerate(subs):
-                for g in range(PASSES):
-                    nc.tensor.matmul_mx(
-                        out=acc[:, n * i : n * (i + 1)],
-                        lhsT=x_codes[:, a, g, P * s : P * (s + 1)].bitcast(E5M2),
-                        lhsT_scale=x_scales[:, a, g, P * s : P * (s + 1)],
-                        rhs=codes["pass", c][:, g, n0 : n0 + n].bitcast(E4M3),
-                        rhs_scale=scales["pass", c][:, g, n0 : n0 + n],
-                        start=(g == 0),
-                        stop=(g == PASSES - 1),
-                    )
-            return acc
+            terms = [(0, c0), (0, c1), (1, neg_c1), (1, c0)]
+            for i in range(first, last):
+                e, factor = terms[i]
+                n = 1024 + CHUNK + 8 * e + c
+                if n0 == 0:
+                    prod = stage.tile([P, HALF], F32, name="prod%d" % i, tag="prod%d" % i, bufs=3)
+                    products[u].append(prod)
+                nc.vector.scalar_tensor_tensor(
+                    out=products[u][i][:, n0:n1],
+                    in0=rot_banks[u][e][:, n0:n1],
+                    scalar=bias[:, n : n + 1],
+                    in1=factor[:, HALF * a + n0 : HALF * a + n1],
+                    op0=ADD,
+                    op1=MULT,
+                )
 
-        def add_bias(u, which, acc):
+        def multiply_pass(u):
+            c, a = divmod(u, HALVES)
+            results[u] = stage.tile([P, 4, SUB, P], F32, name="result", tag="result", bufs=4)
+            return [multiply_tokens(("pass", c), 0, a, pair, "pass") for pair in range(2)]
+
+        def add_pass_bias(u, pair, acc, on_vector):
             c = u // HALVES
-            tag, subs, n0, n = pass_banks(u)[which]
-            by_sub = results[u][:].rearrange("p h s d -> p s h d")[:, subs[0] : subs[-1] + 1]
-            if c < KV:
-                dst, heads = by_sub[:, :, :, 64:128], 4
-            elif which == 0:
-                dst, heads = by_sub[:, :, 0:2, 64:128], 2
+            dst = results[u][:].rearrange("p h s d -> p s h d")[:, 2 * pair : 2 * pair + 2, :, 64:128]
+            sums = acc[:].rearrange("p (s h d) -> p s h d", s=2, h=4)
+            b = bias[:, 256 * c : 256 * (c + 1)].rearrange("p (h d) -> p h d", h=4)
+            if on_vector:
+                add_bias(dst, sums, b)
             else:
-                dst, heads = by_sub[:, :, 2:4, :], 2
-            b = bias[:, 256 * c + n0 : 256 * c + n0 + n].rearrange("p (h d) -> p h d", h=heads)
-            nc.vector.tensor_tensor(
-                out=dst,
-                in0=acc[:].rearrange("p (s h d) -> p s h d", s=len(subs), h=heads),
-                in1=b.unsqueeze(1).to_broadcast([P, len(subs), heads, n // heads]),
-                op=ADD,
-            )
+                nc.scalar.copy(out=dst, in_=sums)
+                nc.gpsimd.tensor_tensor(out=dst, in0=dst, in1=b.unsqueeze(1).to_broadcast(dst.shape), op=ADD)
 
-        def transpose_products(u):
-            c = u // HALVES
+        def transpose_products(u, tags=("rot", "rot")):
             prods = products[u]
-            if c < KV:
-                sums = [(prods[0], prods[2]), (prods[3], prods[1])]
-            else:
-                sums = [(prods[0], prods[1])]
-            per_bank = SUB // len(sums)
+            sums = [(prods[0], prods[2]), (prods[3], prods[1])]
             rotated[u] = []
             for s in range(SUB):
-                if s % per_bank == 0:
-                    r_ps = bank("rot")
+                if s % 2 == 0:
+                    r_ps = bank(tags[s // 2])
                     rotated[u].append(r_ps)
                 for e, terms in enumerate(sums):
-                    n0 = P * (len(sums) * (s % per_bank) + e)
+                    n0 = P * (2 * (s % 2) + e)
                     for i, prod in enumerate(terms):
                         nc.tensor.matmul(
                             r_ps[:, n0 : n0 + P],
@@ -300,79 +343,93 @@ def tile_selfattention_pa_kernel(tc, hidden_states, rope_cache, w_qkv, b_qkv, ou
                             is_transpose=True,
                         )
 
-        def copy_rotated(u):
-            c = u // HALVES
-            heads = 4 if c < KV else 2
-            per_bank = SUB // len(rotated[u])
-            by_sub = results[u][:].rearrange("p h s d -> p s h d")
-            for i, r_ps in enumerate(rotated[u]):
-                dst = by_sub[:, per_bank * i : per_bank * (i + 1), 0:heads, 0:64]
-                nc.scalar.copy(
-                    out=dst.rearrange("p s h (j e) -> p s h j e", e=2),
-                    in_=r_ps[:].rearrange("p (s e h j) -> p s h j e", s=per_bank, e=2, j=32),
-                )
+        def copy_rotated(u, pair):
+            dst = results[u][:].rearrange("p h s d -> p s h d")[:, 2 * pair : 2 * pair + 2, :, 0:64]
+            nc.scalar.copy(
+                out=dst.rearrange("p s h (j e) -> p s h j e", e=2),
+                in_=rotated[u][pair][:].rearrange("p (s e h j) -> p s h j e", s=2, e=2, j=32),
+            )
 
-        def store(u):
+        def store_queries(u, s0=0, s1=SUB):
             c, a = divmod(u, HALVES)
-            tokens = slice(HALF * a, HALF * (a + 1))
-            src = results[u][:].rearrange("p h s d -> p h (s d)")
-            if c < KV:
-                parts = [(out_0[0, 4 * c : 4 * (c + 1), tokens, :], src)]
-            else:
-                parts = [(out_2[0, :, tokens, :], src[:, 2:4]), (out_1[0, :, tokens, :], src[:, 0:2])]
-            for dst, part in parts:
-                nc.sync.dma_start(out=dst.rearrange("h (p s) d -> p h (s d)", s=SUB), in_=part)
+            store(results[u], out_0[0, 4 * c : 4 * (c + 1)], a, s0, s1)
 
-        permute_bias()
-        interleave("rot", 0, 0, nc.vector.tensor_copy)
-        interleave("pass", 0, 0, nc.vector.tensor_copy)
+        tags = ("rot", "rot", "pass", "pass")
+        for s in range(SUB):
+            transpose_x(0, s, tags[s])
         nc.vector.tensor_scalar(out=neg_c1[:], in0=c1, scalar1=-1.0, scalar2=None, op0=MULT)
-        for s, tag in enumerate(("rot", "rot", "pass", "pass")):
-            transpose_x(0, s, tag)
-        spread_bias()
-        interleave("rot", 0, 1, nc.vector.tensor_copy)
-        interleave("pass", 0, 1, nc.scalar.copy)
-        quantize_x(0, 0)
-        quantize_w("rot", 0)
-        quantize_x(0, 1)
-        quantize_w("pass", 0)
-
+        build_token_table()
+        permute_bias()
+        kv_bias_ps, query_bias_ps = spread_bias()
+        interleave_kv(0, nc.vector.tensor_copy, 0, CHUNK)
+        quantize_x(0, 0, PASSES)
+        quantize_w("kv", 0, 1)
+        nc.scalar.copy(out=bias[:, 1024 : 1024 + CHUNK + 16], in_=kv_bias_ps[:, 0 : CHUNK + 16])
+        nc.scalar.copy(out=bias[:, 0:1024], in_=query_bias_ps[:])
+        for s in range(SUB):
+            transpose_x(1, s, tags[s])
+        for s, tag in enumerate(("even", "odd", "even", "odd")):
+            multiply_kv(0, s, 0, tag)
+        interleave_kv(1, nc.vector.tensor_copy, 0, VECTOR_COLUMNS)
+        interleave_kv(1, nc.scalar.copy, VECTOR_COLUMNS, CHUNK)
+        quantize_x(1, 0, 1)
+        quantize_w("kv", 1, 2)
+        quantize_x(1, 1, 2)
+        for s in range(SUB):
+            multiply_kv(0, s, 1)
+        interleave("rot", 0, 0)
+        interleave("rot", 0, 1)
+        for s in range(SUB):
+            add_kv_bias(0, s)
+        for s in range(SUB):
+            for g in range(PASSES):
+                multiply_kv(1, s, g, tags[s])
+        quantize_w(("rot", 0))
+        interleave("pass", 0, 0)
+        interleave("pass", 0, 1)
+        store(values[:, 0], out_2[0], 0)
+        for s in range(SUB):
+            add_kv_bias(1, s)
+            if s == 1:
+                quantize_w(("pass", 0))
+        store(values[:, 1], out_2[0], 1)
+        for a, pair in ((0, 0), (0, 1), (1, 0), (1, 1)):
+            rotate_keys(a, pair)
+        for a in range(HALVES):
+            store(keys[:, a], out_1[0], a)
+        pieces = [(part, c, g) for c in range(1, KV) for part in ("rot", "pass") for g in range(PASSES)]
+        for piece in pieces[:2]:
+            interleave(*piece)
         multiply_rot(0)
-        transpose_x(1, 0, "rot")
-        transpose_x(1, 1, "rot")
-        acc_first = multiply_pass(0, 0)
-        transpose_x(1, 2, "even")
-        transpose_x(1, 3, "odd")
-        acc_second = multiply_pass(0, 1)
-        add_bias(0, 0, acc_first)
-        quantize_x(1, 0)
-        quantize_x(1, 1)
-        add_bias(0, 1, acc_second)
-        transpose_products(0)
-        interleave("rot", 1, 0, nc.scalar.copy)
-        interleave("rot", 1, 1, nc.scalar.copy)
-        multiply_rot(1)
-        quantize_w("rot", 1)
+        form_products(0, 0, 4)
 
-        for u in range(1, UNITS):
+        last = UNITS - 1
+        for u in range(last):
             c = u // HALVES
             part = "rot" if u % HALVES == 0 else "pass"
-            ahead = c + 1 < CHUNKS
+            ahead = c + 1 < KV
+            for piece in pieces[2 + 2 * u : 2 + 2 * u + 1]:
+                interleave(*piece)
+            if u > 0:
+                copy_rotated(u - 1, 0)
+                copy_rotated(u - 1, 1)
+                store_queries(u - 1)
+            for pair, acc in enumerate(multiply_pass(u)):
+                add_pass_bias(u, pair, acc, (u, pair) not in ())
+            for piece in pieces[2 + 2 * u + 1 : 2 + 2 * u + 2]:
+                interleave(*piece)
+            multiply_rot(u + 1)
+            form_products(u + 1, 0, (2 if part == "rot" else 0))
             if ahead:
-                interleave(part, c + 1, 0, nc.scalar.copy)
-            copy_rotated(u - 1)
-            if ahead:
-                interleave(part, c + 1, 1, nc.scalar.copy)
-            store(u - 1)
-            accs = [multiply_pass(u, i) for i in range(len(pass_banks(u)))]
-            for i, acc in enumerate(accs):
-                add_bias(u, i, acc)
-            if ahead:
-                quantize_w(part, c + 1)
-            if u == UNITS - 4:
-                nc.vector.tensor_scalar(out=signed_c1[:], in0=c1, scalar1=sign[:], scalar2=None, op0=MULT)
-            if u + 1 < UNITS:
-                multiply_rot(u + 1)
+                quantize_w((part, c + 1))
+            form_products(u + 1, (2 if part == "rot" else 0), 4)
             transpose_products(u)
-        copy_rotated(UNITS - 1)
-        store(UNITS - 1)
+        for pair in range(2):
+            copy_rotated(last - 1, pair)
+            store_queries(last - 1, 2 * pair, 2 * pair + 2)
+        for pair, acc in enumerate(multiply_pass(last)):
+            add_pass_bias(last, pair, acc, True)
+        transpose_products(last)
+        for pair in range(2):
+            copy_rotated(last, pair)
+            store_queries(last, 2 * pair, 2 * pair + 2)

@@ -61,12 +61,12 @@ def tile_selfattention_pa_kernel(tc, hidden_states, rope_cache, w_qkv, b_qkv, ou
         def load_x(a, s0, s1):
             nc.sync.dma_start(out=x_raw[:, a, s0:s1], in_=x_rows[:, a, s0:s1])
 
+        load_w(KV, 0)
         for s in range(SUB):
             load_x(0, s, s + 1)
-        load_w(KV, 0)
+        load_w(KV, 1)
         load_x(1, 0, 2)
         load_x(1, 2, 4)
-        load_w(KV, 1)
         for c in range(KV):
             for g in range(PASSES):
                 load_w(c, g)
@@ -81,7 +81,7 @@ def tile_selfattention_pa_kernel(tc, hidden_states, rope_cache, w_qkv, b_qkv, ou
                 nc.tensor.transpose(
                     t_ps[:, P * s : P * (s + 1)], cache_rep[:, SUB * a + s].rearrange("p r j -> p (r j)"), ident_f32[:]
                 )
-            nc.vector.tensor_copy(out=table[:, HALF * a : HALF * (a + 1)], in_=t_ps[:])
+            nc.scalar.copy(out=table[:, HALF * a : HALF * (a + 1)], in_=t_ps[:])
         table_pairs = table[:].bitcast(BF16).rearrange("p (n e) -> p n e", e=2)
         c0 = table_pairs[:, :, 0]
         c1 = table_pairs[:, :, 1]
@@ -120,6 +120,15 @@ def tile_selfattention_pa_kernel(tc, hidden_states, rope_cache, w_qkv, b_qkv, ou
                 scales=x_scales[:, a, g0:g1].rearrange("p g n -> p (g n)"),
                 in_=x_group[:, a, g0:g1].rearrange("p g t u -> p (g t u)").bitcast(BF16),
             )
+
+        def quantize_x_pair(a, pair):
+            cols = slice(256 * pair, 256 * (pair + 1))
+            for g in range(PASSES):
+                nc.vector.quantize_mx(
+                    out=x_codes[:, a, g, cols].bitcast(E5M2),
+                    scales=x_scales[:, a, g, cols],
+                    in_=x_group[:, a, g, cols].rearrange("p t u -> p (t u)").bitcast(BF16),
+                )
 
         group = {}
         codes = {}
@@ -323,14 +332,13 @@ def tile_selfattention_pa_kernel(tc, hidden_states, rope_cache, w_qkv, b_qkv, ou
                 nc.scalar.copy(out=dst, in_=sums)
                 nc.gpsimd.tensor_tensor(out=dst, in0=dst, in1=b.unsqueeze(1).to_broadcast(dst.shape), op=ADD)
 
-        def transpose_products(u, tags=("rot", "rot")):
+        def transpose_products(u, pairs=(0, 1)):
             prods = products[u]
             sums = [(prods[0], prods[2]), (prods[3], prods[1])]
-            rotated[u] = []
-            for s in range(SUB):
+            for s in range(2 * pairs[0], 2 * pairs[-1] + 2):
                 if s % 2 == 0:
-                    r_ps = bank(tags[s // 2])
-                    rotated[u].append(r_ps)
+                    r_ps = bank("rot")
+                    rotated[u, s // 2] = r_ps
                 for e, terms in enumerate(sums):
                     n0 = P * (2 * (s % 2) + e)
                     for i, prod in enumerate(terms):
@@ -347,7 +355,7 @@ def tile_selfattention_pa_kernel(tc, hidden_states, rope_cache, w_qkv, b_qkv, ou
             dst = results[u][:].rearrange("p h s d -> p s h d")[:, 2 * pair : 2 * pair + 2, :, 0:64]
             nc.scalar.copy(
                 out=dst.rearrange("p s h (j e) -> p s h j e", e=2),
-                in_=rotated[u][pair][:].rearrange("p (s e h j) -> p s h j e", s=2, e=2, j=32),
+                in_=rotated[u, pair][:].rearrange("p (s e h j) -> p s h j e", s=2, e=2, j=32),
             )
 
         def store_queries(u, s0=0, s1=SUB):
@@ -355,32 +363,34 @@ def tile_selfattention_pa_kernel(tc, hidden_states, rope_cache, w_qkv, b_qkv, ou
             store(results[u], out_0[0, 4 * c : 4 * (c + 1)], a, s0, s1)
 
         tags = ("rot", "rot", "pass", "pass")
-        for s in range(SUB):
-            transpose_x(0, s, tags[s])
-        nc.vector.tensor_scalar(out=neg_c1[:], in0=c1, scalar1=-1.0, scalar2=None, op0=MULT)
         build_token_table()
         permute_bias()
         kv_bias_ps, query_bias_ps = spread_bias()
-        interleave_kv(0, nc.vector.tensor_copy, 0, CHUNK)
-        quantize_x(0, 0, PASSES)
-        quantize_w("kv", 0, 1)
         nc.scalar.copy(out=bias[:, 1024 : 1024 + CHUNK + 16], in_=kv_bias_ps[:, 0 : CHUNK + 16])
         nc.scalar.copy(out=bias[:, 0:1024], in_=query_bias_ps[:])
         for s in range(SUB):
-            transpose_x(1, s, tags[s])
-        for s, tag in enumerate(("even", "odd", "even", "odd")):
-            multiply_kv(0, s, 0, tag)
-        interleave_kv(1, nc.vector.tensor_copy, 0, VECTOR_COLUMNS)
-        interleave_kv(1, nc.scalar.copy, VECTOR_COLUMNS, CHUNK)
-        quantize_x(1, 0, 1)
+            transpose_x(0, s, tags[s])
+        interleave_kv(0, nc.vector.tensor_copy, 0, CHUNK)
+        nc.vector.tensor_scalar(out=neg_c1[:], in0=c1, scalar1=-1.0, scalar2=None, op0=MULT)
+        quantize_w("kv", 0, 1)
+        interleave_kv(1, nc.vector.tensor_copy, 0, CHUNK)
+        quantize_x(0, 0, PASSES)
         quantize_w("kv", 1, 2)
-        quantize_x(1, 1, 2)
-        for s in range(SUB):
-            multiply_kv(0, s, 1)
+        transpose_x(1, 0, tags[0])
+        transpose_x(1, 1, tags[1])
+        for s, tag in enumerate(("even", "odd", "even", "odd")):
+            if s == 0:
+                transpose_x(1, 2, tags[2])
+                transpose_x(1, 3, tags[3])
+            for g in range(PASSES):
+                multiply_kv(0, s, g, tag)
+        quantize_x_pair(1, 0)
         interleave("rot", 0, 0)
         interleave("rot", 0, 1)
         for s in range(SUB):
             add_kv_bias(0, s)
+            if s == 0:
+                quantize_x_pair(1, 1)
         for s in range(SUB):
             for g in range(PASSES):
                 multiply_kv(1, s, g, tags[s])
@@ -390,7 +400,7 @@ def tile_selfattention_pa_kernel(tc, hidden_states, rope_cache, w_qkv, b_qkv, ou
         store(values[:, 0], out_2[0], 0)
         for s in range(SUB):
             add_kv_bias(1, s)
-            if s == 1:
+            if s == 3:
                 quantize_w(("pass", 0))
         store(values[:, 1], out_2[0], 1)
         for a, pair in ((0, 0), (0, 1), (1, 0), (1, 1)):
@@ -401,6 +411,7 @@ def tile_selfattention_pa_kernel(tc, hidden_states, rope_cache, w_qkv, b_qkv, ou
         for piece in pieces[:2]:
             interleave(*piece)
         multiply_rot(0)
+        multiply_rot(1)
         form_products(0, 0, 4)
 
         last = UNITS - 1
@@ -418,7 +429,8 @@ def tile_selfattention_pa_kernel(tc, hidden_states, rope_cache, w_qkv, b_qkv, ou
                 add_pass_bias(u, pair, acc, (u, pair) not in ())
             for piece in pieces[2 + 2 * u + 1 : 2 + 2 * u + 2]:
                 interleave(*piece)
-            multiply_rot(u + 1)
+            if u > 0:
+                multiply_rot(u + 1)
             form_products(u + 1, 0, (2 if part == "rot" else 0))
             if ahead:
                 quantize_w((part, c + 1))

@@ -17,15 +17,23 @@ MULT = mybir.AluOpType.mult
 
 P = 128
 PACK = 4
-PASSES = 2
+K_PASS = P * PACK
+PASSES = HID // K_PASS
 CHUNK = 512
-CHUNKS = 5
-KV = 4
+CHUNKS = QKV // CHUNK
+KV = CHUNKS - 1
+ROT = 64
+PAIRS = ROT // 2
+PART = 4 * ROT
 HALF = 512
-HALVES = 2
-SUB = 4
+HALVES = S // HALF
+TILES = HALF // P
 UNITS = KV * HALVES
-VECTOR_COLUMNS = 384
+BIAS_COLUMNS = KV
+KV_BIAS = KV * PART
+ROT_BIAS = KV_BIAS + CHUNK
+LEAD = 2
+ROT_QUANTIZE_AFTER = 2
 
 
 def tile_selfattention_pa_kernel(tc, hidden_states, rope_cache, w_qkv, b_qkv, out_0, out_1, out_2):
@@ -46,23 +54,23 @@ def tile_selfattention_pa_kernel(tc, hidden_states, rope_cache, w_qkv, b_qkv, ou
         bias_rows = keep.tile([P, CHUNK], BF16)
         nc.vector.memset(bias_rows[:], 0.0)
 
-        cache = keep.tile([P, HALVES, SUB * 64], BF16)
-        nc.scalar.dma_start(out=cache[:], in_=rope_cache[0].rearrange("(a p s) j e -> p a (s j e)", a=HALVES, s=SUB))
+        cache = keep.tile([P, HALVES, TILES * ROT], BF16)
+        nc.scalar.dma_start(out=cache[:], in_=rope_cache[0].rearrange("(a p s) j e -> p a (s j e)", a=HALVES, s=TILES))
         nc.scalar.dma_start(out=bias_rows[0:CHUNKS, :], in_=b_qkv.rearrange("(c n) -> c n", n=CHUNK))
 
         w_raw = keep.tile([P, CHUNKS, PASSES, PACK, CHUNK], BF16)
-        x_raw = keep.tile([P, HALVES, SUB, HID], BF16)
-        x_rows = hidden_states[0].rearrange("(a p s) k -> p a s k", a=HALVES, s=SUB)
+        x_raw = keep.tile([P, HALVES, TILES, HID], BF16)
+        x_rows = hidden_states[0].rearrange("(a p s) k -> p a s k", a=HALVES, s=TILES)
 
         def load_w(c, g):
-            rows = w_qkv[512 * g : 512 * (g + 1), CHUNK * c : CHUNK * (c + 1)]
+            rows = w_qkv[K_PASS * g : K_PASS * (g + 1), CHUNK * c : CHUNK * (c + 1)]
             nc.sync.dma_start(out=w_raw[:, c, g], in_=rows.rearrange("(p t) n -> p t n", t=PACK))
 
         def load_x(a, s0, s1):
             nc.sync.dma_start(out=x_raw[:, a, s0:s1], in_=x_rows[:, a, s0:s1])
 
         load_w(KV, 0)
-        for s in range(SUB):
+        for s in range(TILES):
             load_x(0, s, s + 1)
         load_w(KV, 1)
         load_x(1, 0, 2)
@@ -71,30 +79,34 @@ def tile_selfattention_pa_kernel(tc, hidden_states, rope_cache, w_qkv, b_qkv, ou
             for g in range(PASSES):
                 load_w(c, g)
 
-        cache_rep = keep.tile([P, HALVES * SUB, 4, 32], F32)
-        cache_words = cache[:].rearrange("p a n -> p (a n)").bitcast(F32).rearrange("p (i j) -> p i j", j=32)
-        nc.vector.tensor_copy(out=cache_rep[:], in_=cache_words.unsqueeze(2).to_broadcast([P, HALVES * SUB, 4, 32]))
+        cache_rep = keep.tile([P, HALVES * TILES, 4, PAIRS], F32)
+        cache_words = cache[:].rearrange("p a n -> p (a n)").bitcast(F32).rearrange("p (i j) -> p i j", j=PAIRS)
+        nc.vector.tensor_copy(out=cache_rep[:], in_=cache_words.unsqueeze(2).to_broadcast([P, HALVES * TILES, 4, PAIRS]))
         table = keep.tile([P, S], F32)
         for a in range(HALVES):
-            t_ps = bank("even")
-            for s in range(SUB):
+            table_ps = bank("even")
+            for s in range(TILES):
                 nc.tensor.transpose(
-                    t_ps[:, P * s : P * (s + 1)], cache_rep[:, SUB * a + s].rearrange("p r j -> p (r j)"), ident_f32[:]
+                    table_ps[:, P * s : P * (s + 1)],
+                    cache_rep[:, TILES * a + s].rearrange("p h j -> p (h j)"),
+                    ident_f32[:],
                 )
-            nc.scalar.copy(out=table[:, HALF * a : HALF * (a + 1)], in_=t_ps[:])
+            nc.scalar.copy(out=table[:, HALF * a : HALF * (a + 1)], in_=table_ps[:])
         table_pairs = table[:].bitcast(BF16).rearrange("p (n e) -> p n e", e=2)
         c0 = table_pairs[:, :, 0]
         c1 = table_pairs[:, :, 1]
         neg_c1 = keep.tile([P, S], BF16)
 
-        token_table = keep.tile([P, HALVES * SUB * 32, 2, 2], BF16)
+        token_table = keep.tile([P, HALVES * TILES * PAIRS, 2, 2], BF16)
 
         def build_token_table():
-            pairs = cache[:].rearrange("p a (n e) -> p (a n) e", e=2)
-            nc.vector.tensor_copy(out=token_table[:, :, 0, 0], in_=pairs[:, :, 0])
-            nc.vector.tensor_scalar(out=token_table[:, :, 0, 1], in0=pairs[:, :, 1], scalar1=-1.0, scalar2=None, op0=MULT)
-            nc.vector.tensor_copy(out=token_table[:, :, 1, 0], in_=pairs[:, :, 1])
-            nc.vector.tensor_copy(out=token_table[:, :, 1, 1], in_=pairs[:, :, 0])
+            factors = cache[:].rearrange("p a (n e) -> p (a n) e", e=2)
+            nc.vector.tensor_copy(out=token_table[:, :, 0, 0], in_=factors[:, :, 0])
+            nc.vector.tensor_scalar(
+                out=token_table[:, :, 0, 1], in0=factors[:, :, 1], scalar1=-1.0, scalar2=None, op0=MULT
+            )
+            nc.vector.tensor_copy(out=token_table[:, :, 1, 0], in_=factors[:, :, 1])
+            nc.vector.tensor_copy(out=token_table[:, :, 1, 1], in_=factors[:, :, 0])
 
         x_group = keep.tile([P, HALVES, PASSES, HALF, 2], F32, align_bytes=64)
         x_codes = keep.tile([P, HALVES, PASSES, HALF], U32, align_bytes=64)
@@ -104,174 +116,155 @@ def tile_selfattention_pa_kernel(tc, hidden_states, rope_cache, w_qkv, b_qkv, ou
             words = x_raw[:, a, s].bitcast(F32)
             x_ps = bank(tag)
             for g in range(PASSES):
-                for u in range(2):
-                    i = 2 * g + u
+                for w in range(2):
+                    i = 2 * g + w
                     nc.tensor.transpose(
-                        x_ps[:, P * i : P * (i + 1)], words[:, 256 * g + u : 256 * (g + 1) : 2], ident_f32[:]
+                        x_ps[:, P * i : P * (i + 1)], words[:, 256 * g + w : 256 * (g + 1) : 2], ident_f32[:]
                     )
             nc.scalar.copy(
                 out=x_group[:, a, :, P * s : P * (s + 1), :],
-                in_=x_ps[:].rearrange("p (g u t) -> p g t u", g=PASSES, u=2),
+                in_=x_ps[:].rearrange("p (g w n) -> p g n w", g=PASSES, w=2),
             )
 
-        def quantize_x(a, g0, g1):
+        def quantize_x_half(a):
             nc.vector.quantize_mx(
-                out=x_codes[:, a, g0:g1].rearrange("p g n -> p (g n)").bitcast(E5M2),
-                scales=x_scales[:, a, g0:g1].rearrange("p g n -> p (g n)"),
-                in_=x_group[:, a, g0:g1].rearrange("p g t u -> p (g t u)").bitcast(BF16),
+                out=x_codes[:, a].rearrange("p g n -> p (g n)").bitcast(E5M2),
+                scales=x_scales[:, a].rearrange("p g n -> p (g n)"),
+                in_=x_group[:, a].rearrange("p g n w -> p (g n w)").bitcast(BF16),
             )
 
-        def quantize_x_pair(a, pair):
-            cols = slice(256 * pair, 256 * (pair + 1))
+        def quantize_x_tiles(a, s0):
+            cols = slice(P * s0, P * (s0 + 2))
             for g in range(PASSES):
                 nc.vector.quantize_mx(
                     out=x_codes[:, a, g, cols].bitcast(E5M2),
                     scales=x_scales[:, a, g, cols],
-                    in_=x_group[:, a, g, cols].rearrange("p t u -> p (t u)").bitcast(BF16),
+                    in_=x_group[:, a, g, cols].rearrange("p n w -> p (n w)").bitcast(BF16),
                 )
 
-        group = {}
-        codes = {}
-        scales = {}
-        for name, width in [("kv", CHUNK)] + [((part, c), 256) for c in range(KV) for part in ("rot", "pass")]:
+        w_group = {}
+        w_codes = {}
+        w_scales = {}
+        for name, width in [("kv", CHUNK)] + [((part, c), PART) for c in range(KV) for part in ("rot", "pass")]:
             label = name if name == "kv" else "%s%d" % name
-            codes[name] = keep.tile([P, PASSES, width], U32, name="codes_" + label, align_bytes=64)
-            scales[name] = keep.tile([P, PASSES, width], U8, name="scales_" + label, align_bytes=64)
-        group["kv"] = keep.tile([P, PASSES, CHUNK, PACK], BF16, name="group_kv", align_bytes=64)
+            w_codes[name] = keep.tile([P, PASSES, width], U32, name="codes_" + label, align_bytes=64)
+            w_scales[name] = keep.tile([P, PASSES, width], U8, name="scales_" + label, align_bytes=64)
+        w_group["kv"] = keep.tile([P, PASSES, CHUNK, PACK], BF16, name="group_kv", align_bytes=64)
 
-        def interleave_kv(g, copy, n0, n1):
-            copy(
-                out=group["kv"][:, g, n0:n1].rearrange("p (b i) t -> p b t i", i=4),
-                in_=w_raw[:, KV, g, :, n0:n1].rearrange("p t (b i) -> p b t i", i=4),
+        def interleave_kv(g):
+            nc.vector.tensor_copy(
+                out=w_group["kv"][:, g].rearrange("p (b i) t -> p b t i", i=4),
+                in_=w_raw[:, KV, g].rearrange("p t (b i) -> p b t i", i=4),
             )
 
-        def interleave(part, c, g, copy=nc.scalar.copy):
+        def interleave(part, c, g):
             if g == 0:
-                group[part, c] = stage.tile(
-                    [P, PASSES, 256, PACK], BF16, name="group_" + part, tag="group_" + part, bufs=3, align_bytes=64
+                w_group[part, c] = stage.tile(
+                    [P, PASSES, PART, PACK], BF16, name="group_" + part, tag="group_" + part, bufs=3, align_bytes=64
                 )
-            dst = group[part, c][:, g]
+            dst = w_group[part, c][:, g]
             raw = w_raw[:, c, g]
             if part == "rot":
                 src = raw.rearrange("p t (h r b i e) -> p r e h b t i", r=2, b=8, i=4, e=2)[:, 0]
                 for e in range(2):
-                    copy(out=dst[:, P * e : P * (e + 1)].rearrange("p (h b i) t -> p h b t i", b=8, i=4), in_=src[:, e])
+                    nc.scalar.copy(
+                        out=dst[:, P * e : P * (e + 1)].rearrange("p (h b i) t -> p h b t i", b=8, i=4), in_=src[:, e]
+                    )
             else:
                 src = raw.rearrange("p t (h r b i) -> p r h b t i", r=2, b=16, i=4)[:, 1]
-                copy(out=dst.rearrange("p (h b i) t -> p h b t i", b=16, i=4), in_=src)
+                nc.scalar.copy(out=dst.rearrange("p (h b i) t -> p h b t i", b=16, i=4), in_=src)
 
         def quantize_w(name, g0=0, g1=PASSES):
             nc.vector.quantize_mx(
-                out=codes[name][:, g0:g1].rearrange("p g n -> p (g n)").bitcast(E4M3),
-                scales=scales[name][:, g0:g1].rearrange("p g n -> p (g n)"),
-                in_=group[name][:, g0:g1].rearrange("p g n t -> p (g n t)"),
+                out=w_codes[name][:, g0:g1].rearrange("p g n -> p (g n)").bitcast(E4M3),
+                scales=w_scales[name][:, g0:g1].rearrange("p g n -> p (g n)"),
+                in_=w_group[name][:, g0:g1].rearrange("p g n t -> p (g n t)"),
             )
 
-        bias_perm = keep.tile([P, 2, 4, 32], BF16)
-        bias = keep.tile([P, 1024 + CHUNK + 16], BF16)
+        bias_perm = keep.tile([P, 2, 4, PAIRS], BF16)
+        bias = keep.tile([P, ROT_BIAS + 2 * BIAS_COLUMNS], BF16)
 
         def permute_bias():
-            pairs = bias_rows[:].rearrange("p (h r j e) -> p r e h j", r=2, j=32, e=2)[:, 0]
-            nc.vector.tensor_copy(out=bias_perm[:], in_=pairs)
+            by_parity = bias_rows[:].rearrange("p (h r j e) -> p r e h j", r=2, j=PAIRS, e=2)[:, 0]
+            nc.vector.tensor_copy(out=bias_perm[:], in_=by_parity)
+
+        def row_everywhere(c):
+            return ident_bf[:, c : c + 1].to_broadcast([P, P])
 
         def spread_bias():
-            passing = bias_rows[:].rearrange("p (h r i) -> p r h i", r=2, i=64)[:, 1]
+            passing = bias_rows[:].rearrange("p (h r i) -> p r h i", r=2, i=ROT)[:, 1]
             kv_ps = bank("odd", BF16)
-            nc.tensor.matmul(
-                kv_ps[:, 0:CHUNK],
-                lhsT=ident_bf[:, KV : KV + 1].to_broadcast([P, P]),
-                rhs=bias_rows[:],
-                start=True,
-                stop=True,
-            )
+            nc.tensor.matmul(kv_ps[:, 0:CHUNK], lhsT=row_everywhere(KV), rhs=bias_rows[:], start=True, stop=True)
             for e in range(2):
                 nc.tensor.matmul(
-                    kv_ps[:, CHUNK + 8 * e : CHUNK + 8 * (e + 1)],
+                    kv_ps[:, CHUNK + BIAS_COLUMNS * e : CHUNK + BIAS_COLUMNS * (e + 1)],
                     lhsT=bias_perm[:, e].rearrange("p h j -> p (h j)"),
-                    rhs=ident_bf[:, 0:8],
+                    rhs=ident_bf[:, 0:BIAS_COLUMNS],
                     start=True,
                     stop=True,
                 )
-            q_ps = bank("odd", BF16)
+            query_ps = bank("odd", BF16)
             for c in range(KV):
                 nc.tensor.matmul(
-                    q_ps[:, 256 * c : 256 * (c + 1)].rearrange("p (h i) -> p h i", i=64),
-                    lhsT=ident_bf[:, c : c + 1].to_broadcast([P, P]),
+                    query_ps[:, PART * c : PART * (c + 1)].rearrange("p (h i) -> p h i", i=ROT),
+                    lhsT=row_everywhere(c),
                     rhs=passing,
                     start=True,
                     stop=True,
                 )
-            return kv_ps, q_ps
+            width = CHUNK + 2 * BIAS_COLUMNS
+            nc.scalar.copy(out=bias[:, KV_BIAS : KV_BIAS + width], in_=kv_ps[:, 0:width])
+            nc.scalar.copy(out=bias[:, 0:KV_BIAS], in_=query_ps[:])
 
-        def multiply_tokens(name, n0, a, pair, tag):
-            acc = bank(tag)
-            for i in range(2):
-                tokens = slice(P * (2 * pair + i), P * (2 * pair + i + 1))
-                for g in range(PASSES):
-                    nc.tensor.matmul_mx(
-                        out=acc[:, 256 * i : 256 * (i + 1)],
-                        lhsT=x_codes[:, a, g, tokens].bitcast(E5M2),
-                        lhsT_scale=x_scales[:, a, g, tokens],
-                        rhs=codes[name][:, g, n0 : n0 + 256].bitcast(E4M3),
-                        rhs_scale=scales[name][:, g, n0 : n0 + 256],
-                        start=(g == 0),
-                        stop=(g == PASSES - 1),
-                    )
-            return acc
-
-        def add_bias(dst, acc, b):
-            nc.vector.tensor_tensor(out=dst, in0=acc, in1=b.unsqueeze(1).to_broadcast(dst.shape), op=ADD)
-
-        def store(result, dst, a, s0=0, s1=SUB):
-            rows = dst[:, HALF * a : HALF * (a + 1), :].rearrange("h (p s) d -> p h s d", s=SUB)
+        def store(result, dst, a, s0=0, s1=TILES):
+            rows = dst[:, HALF * a : HALF * (a + 1), :].rearrange("h (p s) d -> p h s d", s=TILES)
             nc.sync.dma_start(out=rows[:, :, s0:s1], in_=result[:, :, s0:s1])
 
-        keys = keep.tile([P, HALVES, 2, SUB, P], F32)
-        values = keep.tile([P, HALVES, 2, SUB, P], F32)
-        unrotated = keep.tile([P, HALVES, SUB, 2, 64], F32)
-        key_bias = bias[:, 1024:1280].rearrange("p (h d) -> p h d", h=2)
-        value_bias = bias[:, 1280:1536].rearrange("p (h d) -> p h d", h=2)
-
+        keys = keep.tile([P, HALVES, 2, TILES, P], F32)
+        values = keep.tile([P, HALVES, 2, TILES, P], F32)
+        unrotated = keep.tile([P, HALVES, TILES, 2, ROT], F32)
+        key_bias = bias[:, KV_BIAS : KV_BIAS + 2 * P].rearrange("p (h d) -> p h d", h=2)
+        value_bias = bias[:, KV_BIAS + 2 * P : ROT_BIAS].rearrange("p (h d) -> p h d", h=2)
         kv_banks = {}
 
-        def multiply_kv(a, s, g, tag=None):
-            if g == 0:
-                kv_banks[a, s] = bank(tag)
+        def multiply_kv(a, s, tag):
+            kv_banks[a, s] = bank(tag)
             tokens = slice(P * s, P * (s + 1))
-            nc.tensor.matmul_mx(
-                out=kv_banks[a, s][:],
-                lhsT=x_codes[:, a, g, tokens].bitcast(E5M2),
-                lhsT_scale=x_scales[:, a, g, tokens],
-                rhs=codes["kv"][:, g].bitcast(E4M3),
-                rhs_scale=scales["kv"][:, g],
-                start=(g == 0),
-                stop=(g == PASSES - 1),
-            )
+            for g in range(PASSES):
+                nc.tensor.matmul_mx(
+                    out=kv_banks[a, s][:],
+                    lhsT=x_codes[:, a, g, tokens].bitcast(E5M2),
+                    lhsT_scale=x_scales[:, a, g, tokens],
+                    rhs=w_codes["kv"][:, g].bitcast(E4M3),
+                    rhs_scale=w_scales["kv"][:, g],
+                    start=(g == 0),
+                    stop=(g == PASSES - 1),
+                )
 
         def add_kv_bias(a, s):
-            acc = kv_banks[a, s][:].rearrange("p (h d) -> p h d", h=4)
-            nc.vector.tensor_tensor(out=unrotated[:, a, s], in0=acc[:, 0:2, 0:64], in1=key_bias[:, :, 0:64], op=ADD)
+            sums = kv_banks[a, s][:].rearrange("p (h d) -> p h d", h=4)
+            nc.vector.tensor_tensor(out=unrotated[:, a, s], in0=sums[:, 0:2, 0:ROT], in1=key_bias[:, :, 0:ROT], op=ADD)
             nc.vector.tensor_tensor(
-                out=keys[:, a, :, s, 64:128], in0=acc[:, 0:2, 64:128], in1=key_bias[:, :, 64:128], op=ADD
+                out=keys[:, a, :, s, ROT:P], in0=sums[:, 0:2, ROT:P], in1=key_bias[:, :, ROT:P], op=ADD
             )
-            nc.vector.tensor_tensor(out=values[:, a, :, s], in0=acc[:, 2:4], in1=value_bias, op=ADD)
+            nc.vector.tensor_tensor(out=values[:, a, :, s], in0=sums[:, 2:4], in1=value_bias, op=ADD)
 
-        def rotate_keys(a, pair):
-            subs = slice(2 * pair, 2 * pair + 2)
-            shape = [P, 2, 2, 32, 2, 2]
+        def rotate_keys(a, s0):
+            tiles = slice(s0, s0 + 2)
+            shape = [P, 2, 2, PAIRS, 2, 2]
             terms = stage.tile(shape, F32, name="terms", tag="terms")
-            factors = token_table[:].rearrange("p (a s j) y e -> p a s j y e", a=HALVES, j=32)[:, a, subs]
+            factors = token_table[:].rearrange("p (a s j) y e -> p a s j y e", a=HALVES, j=PAIRS)[:, a, tiles]
             nc.gpsimd.tensor_tensor(
                 out=terms[:],
-                in0=unrotated[:, a, subs].rearrange("p s h (j e) -> p s h j e", e=2).unsqueeze(4).to_broadcast(shape),
+                in0=unrotated[:, a, tiles].rearrange("p s h (j e) -> p s h j e", e=2).unsqueeze(4).to_broadcast(shape),
                 in1=factors.unsqueeze(2).to_broadcast(shape),
                 op=MULT,
             )
-            by_term = terms[:].rearrange("p s h j y e -> p s h (j y) e")
+            by_output = terms[:].rearrange("p s h j y e -> p s h (j y) e")
             nc.gpsimd.tensor_tensor(
-                out=keys[:, a].rearrange("p h s d -> p s h d")[:, subs, :, 0:64],
-                in0=by_term[:, :, :, :, 0],
-                in1=by_term[:, :, :, :, 1],
+                out=keys[:, a].rearrange("p h s d -> p s h d")[:, tiles, :, 0:ROT],
+                in0=by_output[:, :, :, :, 0],
+                in1=by_output[:, :, :, :, 1],
                 op=ADD,
             )
 
@@ -289,8 +282,8 @@ def tile_selfattention_pa_kernel(tc, hidden_states, rope_cache, w_qkv, b_qkv, ou
                 for g in range(PASSES):
                     nc.tensor.matmul_mx(
                         out=acc[:],
-                        lhsT=codes["rot", c][:, g, P * e : P * (e + 1)].bitcast(E4M3),
-                        lhsT_scale=scales["rot", c][:, g, P * e : P * (e + 1)],
+                        lhsT=w_codes["rot", c][:, g, P * e : P * (e + 1)].bitcast(E4M3),
+                        lhsT_scale=w_scales["rot", c][:, g, P * e : P * (e + 1)],
                         rhs=x_codes[:, a, g].bitcast(E5M2),
                         rhs_scale=x_scales[:, a, g],
                         start=(g == 0),
@@ -298,117 +291,120 @@ def tile_selfattention_pa_kernel(tc, hidden_states, rope_cache, w_qkv, b_qkv, ou
                     )
                 rot_banks[u].append(acc)
 
-        def form_products(u, first, last, n0=0, n1=HALF):
+        def form_products(u, first, stop):
             c, a = divmod(u, HALVES)
-            terms = [(0, c0), (0, c1), (1, neg_c1), (1, c0)]
-            for i in range(first, last):
-                e, factor = terms[i]
-                n = 1024 + CHUNK + 8 * e + c
-                if n0 == 0:
-                    prod = stage.tile([P, HALF], F32, name="prod%d" % i, tag="prod%d" % i, bufs=3)
-                    products[u].append(prod)
+            for i in range(first, stop):
+                e, factor = ((0, c0), (0, c1), (1, neg_c1), (1, c0))[i]
+                n = ROT_BIAS + BIAS_COLUMNS * e + c
+                product = stage.tile([P, HALF], F32, name="prod%d" % i, tag="prod%d" % i, bufs=3)
+                products[u].append(product)
                 nc.vector.scalar_tensor_tensor(
-                    out=products[u][i][:, n0:n1],
-                    in0=rot_banks[u][e][:, n0:n1],
+                    out=product[:],
+                    in0=rot_banks[u][e][:],
                     scalar=bias[:, n : n + 1],
-                    in1=factor[:, HALF * a + n0 : HALF * a + n1],
+                    in1=factor[:, HALF * a : HALF * (a + 1)],
                     op0=ADD,
                     op1=MULT,
                 )
 
-        def multiply_pass(u):
+        def pass_channels(u):
             c, a = divmod(u, HALVES)
-            results[u] = stage.tile([P, 4, SUB, P], F32, name="result", tag="result", bufs=4)
-            return [multiply_tokens(("pass", c), 0, a, pair, "pass") for pair in range(2)]
+            results[u] = stage.tile([P, 4, TILES, P], F32, name="result", tag="result", bufs=4)
+            banks = []
+            for s0 in range(0, TILES, 2):
+                acc = bank("pass")
+                for i in range(2):
+                    tokens = slice(P * (s0 + i), P * (s0 + i + 1))
+                    for g in range(PASSES):
+                        nc.tensor.matmul_mx(
+                            out=acc[:, PART * i : PART * (i + 1)],
+                            lhsT=x_codes[:, a, g, tokens].bitcast(E5M2),
+                            lhsT_scale=x_scales[:, a, g, tokens],
+                            rhs=w_codes["pass", c][:, g].bitcast(E4M3),
+                            rhs_scale=w_scales["pass", c][:, g],
+                            start=(g == 0),
+                            stop=(g == PASSES - 1),
+                        )
+                banks.append((s0, acc))
+            pass_bias = bias[:, PART * c : PART * (c + 1)].rearrange("p (h d) -> p h d", h=4)
+            for s0, acc in banks:
+                nc.vector.tensor_tensor(
+                    out=results[u][:].rearrange("p h s d -> p s h d")[:, s0 : s0 + 2, :, ROT:P],
+                    in0=acc[:].rearrange("p (s h d) -> p s h d", s=2, h=4),
+                    in1=pass_bias.unsqueeze(1).to_broadcast([P, 2, 4, ROT]),
+                    op=ADD,
+                )
 
-        def add_pass_bias(u, pair, acc, on_vector):
-            c = u // HALVES
-            dst = results[u][:].rearrange("p h s d -> p s h d")[:, 2 * pair : 2 * pair + 2, :, 64:128]
-            sums = acc[:].rearrange("p (s h d) -> p s h d", s=2, h=4)
-            b = bias[:, 256 * c : 256 * (c + 1)].rearrange("p (h d) -> p h d", h=4)
-            if on_vector:
-                add_bias(dst, sums, b)
-            else:
-                nc.scalar.copy(out=dst, in_=sums)
-                nc.gpsimd.tensor_tensor(out=dst, in0=dst, in1=b.unsqueeze(1).to_broadcast(dst.shape), op=ADD)
-
-        def transpose_products(u, pairs=(0, 1)):
-            prods = products[u]
-            sums = [(prods[0], prods[2]), (prods[3], prods[1])]
-            for s in range(2 * pairs[0], 2 * pairs[-1] + 2):
+        def transpose_products(u):
+            sums = ((products[u][0], products[u][2]), (products[u][3], products[u][1]))
+            for s in range(TILES):
                 if s % 2 == 0:
-                    r_ps = bank("rot")
-                    rotated[u, s // 2] = r_ps
-                for e, terms in enumerate(sums):
-                    n0 = P * (2 * (s % 2) + e)
-                    for i, prod in enumerate(terms):
+                    rotated[u, s] = bank("rot")
+                for y, addends in enumerate(sums):
+                    n0 = P * (2 * (s % 2) + y)
+                    for i, product in enumerate(addends):
                         nc.tensor.matmul(
-                            r_ps[:, n0 : n0 + P],
-                            lhsT=prod[:, P * s : P * (s + 1)],
+                            rotated[u, s - s % 2][:, n0 : n0 + P],
+                            lhsT=product[:, P * s : P * (s + 1)],
                             rhs=ident_f32[:],
                             start=(i == 0),
                             stop=(i == 1),
                             is_transpose=True,
                         )
 
-        def copy_rotated(u, pair):
-            dst = results[u][:].rearrange("p h s d -> p s h d")[:, 2 * pair : 2 * pair + 2, :, 0:64]
+        def copy_rotated(u, s0):
+            dst = results[u][:].rearrange("p h s d -> p s h d")[:, s0 : s0 + 2, :, 0:ROT]
             nc.scalar.copy(
-                out=dst.rearrange("p s h (j e) -> p s h j e", e=2),
-                in_=rotated[u, pair][:].rearrange("p (s e h j) -> p s h j e", s=2, e=2, j=32),
+                out=dst.rearrange("p s h (j y) -> p s h j y", y=2),
+                in_=rotated[u, s0][:].rearrange("p (s y h j) -> p s h j y", s=2, y=2, j=PAIRS),
             )
 
-        def store_queries(u, s0=0, s1=SUB):
+        def store_queries(u, s0=0, s1=TILES):
             c, a = divmod(u, HALVES)
             store(results[u], out_0[0, 4 * c : 4 * (c + 1)], a, s0, s1)
 
-        tags = ("rot", "rot", "pass", "pass")
+        free_tags = ("rot", "rot", "pass", "pass")
         build_token_table()
         permute_bias()
-        kv_bias_ps, query_bias_ps = spread_bias()
-        nc.scalar.copy(out=bias[:, 1024 : 1024 + CHUNK + 16], in_=kv_bias_ps[:, 0 : CHUNK + 16])
-        nc.scalar.copy(out=bias[:, 0:1024], in_=query_bias_ps[:])
-        for s in range(SUB):
-            transpose_x(0, s, tags[s])
-        interleave_kv(0, nc.vector.tensor_copy, 0, CHUNK)
+        for s in range(TILES):
+            transpose_x(0, s, free_tags[s])
+        spread_bias()
+        interleave_kv(0)
         nc.vector.tensor_scalar(out=neg_c1[:], in0=c1, scalar1=-1.0, scalar2=None, op0=MULT)
         quantize_w("kv", 0, 1)
-        interleave_kv(1, nc.vector.tensor_copy, 0, CHUNK)
-        quantize_x(0, 0, PASSES)
+        interleave_kv(1)
+        quantize_x_half(0)
         quantize_w("kv", 1, 2)
-        transpose_x(1, 0, tags[0])
-        transpose_x(1, 1, tags[1])
-        for s, tag in enumerate(("even", "odd", "even", "odd")):
-            if s == 0:
-                transpose_x(1, 2, tags[2])
-                transpose_x(1, 3, tags[3])
-            for g in range(PASSES):
-                multiply_kv(0, s, g, tag)
-        quantize_x_pair(1, 0)
+        for s in range(TILES):
+            transpose_x(1, s, free_tags[s])
+
+        for s in range(TILES):
+            multiply_kv(0, s, ("even", "odd")[s % 2])
+        quantize_x_tiles(1, 0)
         interleave("rot", 0, 0)
         interleave("rot", 0, 1)
-        for s in range(SUB):
+        add_kv_bias(0, 0)
+        quantize_x_tiles(1, 2)
+        for s in range(1, TILES):
             add_kv_bias(0, s)
-            if s == 0:
-                quantize_x_pair(1, 1)
-        for s in range(SUB):
-            for g in range(PASSES):
-                multiply_kv(1, s, g, tags[s])
+        for s in range(TILES):
+            multiply_kv(1, s, free_tags[s])
         quantize_w(("rot", 0))
         interleave("pass", 0, 0)
         interleave("pass", 0, 1)
         store(values[:, 0], out_2[0], 0)
-        for s in range(SUB):
+        for s in range(TILES):
             add_kv_bias(1, s)
-            if s == 3:
-                quantize_w(("pass", 0))
+        quantize_w(("pass", 0))
         store(values[:, 1], out_2[0], 1)
-        for a, pair in ((0, 0), (0, 1), (1, 0), (1, 1)):
-            rotate_keys(a, pair)
+        for a in range(HALVES):
+            for s0 in range(0, TILES, 2):
+                rotate_keys(a, s0)
         for a in range(HALVES):
             store(keys[:, a], out_1[0], a)
+
         pieces = [(part, c, g) for c in range(1, KV) for part in ("rot", "pass") for g in range(PASSES)]
-        for piece in pieces[:2]:
+        for piece in pieces[:LEAD]:
             interleave(*piece)
         multiply_rot(0)
         multiply_rot(1)
@@ -416,32 +412,32 @@ def tile_selfattention_pa_kernel(tc, hidden_states, rope_cache, w_qkv, b_qkv, ou
 
         last = UNITS - 1
         for u in range(last):
-            c = u // HALVES
-            part = "rot" if u % HALVES == 0 else "pass"
-            ahead = c + 1 < KV
-            for piece in pieces[2 + 2 * u : 2 + 2 * u + 1]:
-                interleave(*piece)
+            part = ("rot", "pass")[u % HALVES]
+            next_chunk = u // HALVES + 1
+            round_pieces = pieces[LEAD + 2 * u : LEAD + 2 * u + 2]
+            if round_pieces:
+                interleave(*round_pieces[0])
             if u > 0:
                 copy_rotated(u - 1, 0)
-                copy_rotated(u - 1, 1)
+                copy_rotated(u - 1, 2)
                 store_queries(u - 1)
-            for pair, acc in enumerate(multiply_pass(u)):
-                add_pass_bias(u, pair, acc, (u, pair) not in ())
-            for piece in pieces[2 + 2 * u + 1 : 2 + 2 * u + 2]:
-                interleave(*piece)
+            pass_channels(u)
+            if round_pieces:
+                interleave(*round_pieces[1])
             if u > 0:
                 multiply_rot(u + 1)
-            form_products(u + 1, 0, (2 if part == "rot" else 0))
-            if ahead:
-                quantize_w((part, c + 1))
-            form_products(u + 1, (2 if part == "rot" else 0), 4)
+            before = ROT_QUANTIZE_AFTER if part == "rot" else 0
+            form_products(u + 1, 0, before)
+            if next_chunk < KV:
+                quantize_w((part, next_chunk))
+            form_products(u + 1, before, 4)
             transpose_products(u)
-        for pair in range(2):
-            copy_rotated(last - 1, pair)
-            store_queries(last - 1, 2 * pair, 2 * pair + 2)
-        for pair, acc in enumerate(multiply_pass(last)):
-            add_pass_bias(last, pair, acc, True)
+
+        for s0 in range(0, TILES, 2):
+            copy_rotated(last - 1, s0)
+            store_queries(last - 1, s0, s0 + 2)
+        pass_channels(last)
         transpose_products(last)
-        for pair in range(2):
-            copy_rotated(last, pair)
-            store_queries(last, 2 * pair, 2 * pair + 2)
+        for s0 in range(0, TILES, 2):
+            copy_rotated(last, s0)
+            store_queries(last, s0, s0 + 2)

from contextlib import ExitStack

import concourse.mybir as mybir
from concourse.masks import make_identity

S, HID, QKV = 1024, 1024, 2560
FLOPS = 2 * S * HID * QKV

F32 = mybir.dt.float32
BF16 = mybir.dt.bfloat16
U32 = mybir.dt.uint32
U8 = mybir.dt.uint8
E5M2 = mybir.dt.float8_e5m2_x4
E4M3 = mybir.dt.float8_e4m3fn_x4
ADD = mybir.AluOpType.add
MULT = mybir.AluOpType.mult

P = 128
PACK = 4
K_PASS = P * PACK
PASSES = HID // K_PASS
CHUNK = 512
CHUNKS = QKV // CHUNK
KV = CHUNKS - 1
ROT = 64
PAIRS = ROT // 2
PART = 4 * ROT
HALF = 512
HALVES = S // HALF
TILES = HALF // P
UNITS = KV * HALVES
BIAS_COLUMNS = KV
KV_BIAS = KV * PART
ROT_BIAS = KV_BIAS + CHUNK
LEAD = 2
ROT_QUANTIZE_AFTER = 2


def tile_selfattention_pa_kernel(tc, hidden_states, rope_cache, w_qkv, b_qkv, out_0, out_1, out_2):
    nc = tc.nc
    with ExitStack() as ctx:
        keep = ctx.enter_context(tc.tile_pool(name="keep", bufs=1))
        stage = ctx.enter_context(tc.tile_pool(name="stage", bufs=2))
        psum = ctx.enter_context(tc.psum_pool(name="psum", bufs=2))
        ctx.enter_context(tc.manual_schedule())

        def bank(tag, dtype=F32):
            return psum.tile([P, 512 if dtype == F32 else 1024], dtype, name=tag, tag=tag)

        ident_f32 = keep.tile([P, P], F32)
        make_identity(nc, ident_f32[:])
        ident_bf = keep.tile([P, P], BF16)
        make_identity(nc, ident_bf[:])
        bias_rows = keep.tile([P, CHUNK], BF16)
        nc.vector.memset(bias_rows[:], 0.0)

        cache = keep.tile([P, HALVES, TILES * ROT], BF16)
        nc.scalar.dma_start(out=cache[:], in_=rope_cache[0].rearrange("(a p s) j e -> p a (s j e)", a=HALVES, s=TILES))
        nc.scalar.dma_start(out=bias_rows[0:CHUNKS, :], in_=b_qkv.rearrange("(c n) -> c n", n=CHUNK))

        w_raw = keep.tile([P, CHUNKS, PASSES, PACK, CHUNK], BF16)
        x_raw = keep.tile([P, HALVES, TILES, HID], BF16)
        x_rows = hidden_states[0].rearrange("(a p s) k -> p a s k", a=HALVES, s=TILES)

        def load_w(c, g):
            rows = w_qkv[K_PASS * g : K_PASS * (g + 1), CHUNK * c : CHUNK * (c + 1)]
            nc.sync.dma_start(out=w_raw[:, c, g], in_=rows.rearrange("(p t) n -> p t n", t=PACK))

        def load_x(a, s0, s1):
            nc.sync.dma_start(out=x_raw[:, a, s0:s1], in_=x_rows[:, a, s0:s1])

        load_w(KV, 0)
        for s in range(TILES):
            load_x(0, s, s + 1)
        load_w(KV, 1)
        load_x(1, 0, 2)
        load_x(1, 2, 4)
        for c in range(KV):
            for g in range(PASSES):
                load_w(c, g)

        cache_rep = keep.tile([P, HALVES * TILES, 4, PAIRS], F32)
        cache_words = cache[:].rearrange("p a n -> p (a n)").bitcast(F32).rearrange("p (i j) -> p i j", j=PAIRS)
        nc.vector.tensor_copy(out=cache_rep[:], in_=cache_words.unsqueeze(2).to_broadcast([P, HALVES * TILES, 4, PAIRS]))
        table = keep.tile([P, S], F32)
        for a in range(HALVES):
            table_ps = bank("even")
            for s in range(TILES):
                nc.tensor.transpose(
                    table_ps[:, P * s : P * (s + 1)],
                    cache_rep[:, TILES * a + s].rearrange("p h j -> p (h j)"),
                    ident_f32[:],
                )
            nc.scalar.copy(out=table[:, HALF * a : HALF * (a + 1)], in_=table_ps[:])
        table_pairs = table[:].bitcast(BF16).rearrange("p (n e) -> p n e", e=2)
        c0 = table_pairs[:, :, 0]
        c1 = table_pairs[:, :, 1]
        neg_c1 = keep.tile([P, S], BF16)

        token_table = keep.tile([P, HALVES * TILES * PAIRS, 2, 2], BF16)

        def build_token_table():
            factors = cache[:].rearrange("p a (n e) -> p (a n) e", e=2)
            nc.vector.tensor_copy(out=token_table[:, :, 0, 0], in_=factors[:, :, 0])
            nc.vector.tensor_scalar(
                out=token_table[:, :, 0, 1], in0=factors[:, :, 1], scalar1=-1.0, scalar2=None, op0=MULT
            )
            nc.vector.tensor_copy(out=token_table[:, :, 1, 0], in_=factors[:, :, 1])
            nc.vector.tensor_copy(out=token_table[:, :, 1, 1], in_=factors[:, :, 0])

        x_group = keep.tile([P, HALVES, PASSES, HALF, 2], F32, align_bytes=64)
        x_codes = keep.tile([P, HALVES, PASSES, HALF], U32, align_bytes=64)
        x_scales = keep.tile([P, HALVES, PASSES, HALF], U8, align_bytes=64)

        def transpose_x(a, s, tag):
            words = x_raw[:, a, s].bitcast(F32)
            x_ps = bank(tag)
            for g in range(PASSES):
                for w in range(2):
                    i = 2 * g + w
                    nc.tensor.transpose(
                        x_ps[:, P * i : P * (i + 1)], words[:, 256 * g + w : 256 * (g + 1) : 2], ident_f32[:]
                    )
            nc.scalar.copy(
                out=x_group[:, a, :, P * s : P * (s + 1), :],
                in_=x_ps[:].rearrange("p (g w n) -> p g n w", g=PASSES, w=2),
            )

        def quantize_x_half(a):
            nc.vector.quantize_mx(
                out=x_codes[:, a].rearrange("p g n -> p (g n)").bitcast(E5M2),
                scales=x_scales[:, a].rearrange("p g n -> p (g n)"),
                in_=x_group[:, a].rearrange("p g n w -> p (g n w)").bitcast(BF16),
            )

        def quantize_x_tiles(a, s0):
            cols = slice(P * s0, P * (s0 + 2))
            for g in range(PASSES):
                nc.vector.quantize_mx(
                    out=x_codes[:, a, g, cols].bitcast(E5M2),
                    scales=x_scales[:, a, g, cols],
                    in_=x_group[:, a, g, cols].rearrange("p n w -> p (n w)").bitcast(BF16),
                )

        w_group = {}
        w_codes = {}
        w_scales = {}
        for name, width in [("kv", CHUNK)] + [((part, c), PART) for c in range(KV) for part in ("rot", "pass")]:
            label = name if name == "kv" else "%s%d" % name
            w_codes[name] = keep.tile([P, PASSES, width], U32, name="codes_" + label, align_bytes=64)
            w_scales[name] = keep.tile([P, PASSES, width], U8, name="scales_" + label, align_bytes=64)
        w_group["kv"] = keep.tile([P, PASSES, CHUNK, PACK], BF16, name="group_kv", align_bytes=64)

        def interleave_kv(g):
            nc.vector.tensor_copy(
                out=w_group["kv"][:, g].rearrange("p (b i) t -> p b t i", i=4),
                in_=w_raw[:, KV, g].rearrange("p t (b i) -> p b t i", i=4),
            )

        def interleave(part, c, g):
            if g == 0:
                w_group[part, c] = stage.tile(
                    [P, PASSES, PART, PACK], BF16, name="group_" + part, tag="group_" + part, bufs=3, align_bytes=64
                )
            dst = w_group[part, c][:, g]
            raw = w_raw[:, c, g]
            if part == "rot":
                src = raw.rearrange("p t (h r b i e) -> p r e h b t i", r=2, b=8, i=4, e=2)[:, 0]
                for e in range(2):
                    nc.scalar.copy(
                        out=dst[:, P * e : P * (e + 1)].rearrange("p (h b i) t -> p h b t i", b=8, i=4), in_=src[:, e]
                    )
            else:
                src = raw.rearrange("p t (h r b i) -> p r h b t i", r=2, b=16, i=4)[:, 1]
                nc.scalar.copy(out=dst.rearrange("p (h b i) t -> p h b t i", b=16, i=4), in_=src)

        def quantize_w(name, g0=0, g1=PASSES):
            nc.vector.quantize_mx(
                out=w_codes[name][:, g0:g1].rearrange("p g n -> p (g n)").bitcast(E4M3),
                scales=w_scales[name][:, g0:g1].rearrange("p g n -> p (g n)"),
                in_=w_group[name][:, g0:g1].rearrange("p g n t -> p (g n t)"),
            )

        bias_perm = keep.tile([P, 2, 4, PAIRS], BF16)
        bias = keep.tile([P, ROT_BIAS + 2 * BIAS_COLUMNS], BF16)

        def permute_bias():
            by_parity = bias_rows[:].rearrange("p (h r j e) -> p r e h j", r=2, j=PAIRS, e=2)[:, 0]
            nc.vector.tensor_copy(out=bias_perm[:], in_=by_parity)

        def row_everywhere(c):
            return ident_bf[:, c : c + 1].to_broadcast([P, P])

        def spread_bias():
            passing = bias_rows[:].rearrange("p (h r i) -> p r h i", r=2, i=ROT)[:, 1]
            kv_ps = bank("odd", BF16)
            nc.tensor.matmul(kv_ps[:, 0:CHUNK], lhsT=row_everywhere(KV), rhs=bias_rows[:], start=True, stop=True)
            for e in range(2):
                nc.tensor.matmul(
                    kv_ps[:, CHUNK + BIAS_COLUMNS * e : CHUNK + BIAS_COLUMNS * (e + 1)],
                    lhsT=bias_perm[:, e].rearrange("p h j -> p (h j)"),
                    rhs=ident_bf[:, 0:BIAS_COLUMNS],
                    start=True,
                    stop=True,
                )
            query_ps = bank("odd", BF16)
            for c in range(KV):
                nc.tensor.matmul(
                    query_ps[:, PART * c : PART * (c + 1)].rearrange("p (h i) -> p h i", i=ROT),
                    lhsT=row_everywhere(c),
                    rhs=passing,
                    start=True,
                    stop=True,
                )
            width = CHUNK + 2 * BIAS_COLUMNS
            nc.scalar.copy(out=bias[:, KV_BIAS : KV_BIAS + width], in_=kv_ps[:, 0:width])
            nc.scalar.copy(out=bias[:, 0:KV_BIAS], in_=query_ps[:])

        def store(result, dst, a, s0=0, s1=TILES):
            rows = dst[:, HALF * a : HALF * (a + 1), :].rearrange("h (p s) d -> p h s d", s=TILES)
            nc.sync.dma_start(out=rows[:, :, s0:s1], in_=result[:, :, s0:s1])

        keys = keep.tile([P, HALVES, 2, TILES, P], F32)
        values = keep.tile([P, HALVES, 2, TILES, P], F32)
        unrotated = keep.tile([P, HALVES, TILES, 2, ROT], F32)
        key_bias = bias[:, KV_BIAS : KV_BIAS + 2 * P].rearrange("p (h d) -> p h d", h=2)
        value_bias = bias[:, KV_BIAS + 2 * P : ROT_BIAS].rearrange("p (h d) -> p h d", h=2)
        kv_banks = {}

        def multiply_kv(a, s, tag):
            kv_banks[a, s] = bank(tag)
            tokens = slice(P * s, P * (s + 1))
            for g in range(PASSES):
                nc.tensor.matmul_mx(
                    out=kv_banks[a, s][:],
                    lhsT=x_codes[:, a, g, tokens].bitcast(E5M2),
                    lhsT_scale=x_scales[:, a, g, tokens],
                    rhs=w_codes["kv"][:, g].bitcast(E4M3),
                    rhs_scale=w_scales["kv"][:, g],
                    start=(g == 0),
                    stop=(g == PASSES - 1),
                )

        def add_kv_bias(a, s):
            sums = kv_banks[a, s][:].rearrange("p (h d) -> p h d", h=4)
            nc.vector.tensor_tensor(out=unrotated[:, a, s], in0=sums[:, 0:2, 0:ROT], in1=key_bias[:, :, 0:ROT], op=ADD)
            nc.vector.tensor_tensor(
                out=keys[:, a, :, s, ROT:P], in0=sums[:, 0:2, ROT:P], in1=key_bias[:, :, ROT:P], op=ADD
            )
            nc.vector.tensor_tensor(out=values[:, a, :, s], in0=sums[:, 2:4], in1=value_bias, op=ADD)

        def rotate_keys(a, s0):
            tiles = slice(s0, s0 + 2)
            shape = [P, 2, 2, PAIRS, 2, 2]
            terms = stage.tile(shape, F32, name="terms", tag="terms")
            factors = token_table[:].rearrange("p (a s j) y e -> p a s j y e", a=HALVES, j=PAIRS)[:, a, tiles]
            nc.gpsimd.tensor_tensor(
                out=terms[:],
                in0=unrotated[:, a, tiles].rearrange("p s h (j e) -> p s h j e", e=2).unsqueeze(4).to_broadcast(shape),
                in1=factors.unsqueeze(2).to_broadcast(shape),
                op=MULT,
            )
            by_output = terms[:].rearrange("p s h j y e -> p s h (j y) e")
            nc.gpsimd.tensor_tensor(
                out=keys[:, a].rearrange("p h s d -> p s h d")[:, tiles, :, 0:ROT],
                in0=by_output[:, :, :, :, 0],
                in1=by_output[:, :, :, :, 1],
                op=ADD,
            )

        rot_banks = {}
        products = {}
        results = {}
        rotated = {}

        def multiply_rot(u):
            c, a = divmod(u, HALVES)
            rot_banks[u] = []
            products[u] = []
            for e, tag in enumerate(("even", "odd")):
                acc = bank(tag)
                for g in range(PASSES):
                    nc.tensor.matmul_mx(
                        out=acc[:],
                        lhsT=w_codes["rot", c][:, g, P * e : P * (e + 1)].bitcast(E4M3),
                        lhsT_scale=w_scales["rot", c][:, g, P * e : P * (e + 1)],
                        rhs=x_codes[:, a, g].bitcast(E5M2),
                        rhs_scale=x_scales[:, a, g],
                        start=(g == 0),
                        stop=(g == PASSES - 1),
                    )
                rot_banks[u].append(acc)

        def form_products(u, first, stop):
            c, a = divmod(u, HALVES)
            for i in range(first, stop):
                e, factor = ((0, c0), (0, c1), (1, neg_c1), (1, c0))[i]
                n = ROT_BIAS + BIAS_COLUMNS * e + c
                product = stage.tile([P, HALF], F32, name="prod%d" % i, tag="prod%d" % i, bufs=3)
                products[u].append(product)
                nc.vector.scalar_tensor_tensor(
                    out=product[:],
                    in0=rot_banks[u][e][:],
                    scalar=bias[:, n : n + 1],
                    in1=factor[:, HALF * a : HALF * (a + 1)],
                    op0=ADD,
                    op1=MULT,
                )

        def pass_channels(u):
            c, a = divmod(u, HALVES)
            results[u] = stage.tile([P, 4, TILES, P], F32, name="result", tag="result", bufs=4)
            banks = []
            for s0 in range(0, TILES, 2):
                acc = bank("pass")
                for i in range(2):
                    tokens = slice(P * (s0 + i), P * (s0 + i + 1))
                    for g in range(PASSES):
                        nc.tensor.matmul_mx(
                            out=acc[:, PART * i : PART * (i + 1)],
                            lhsT=x_codes[:, a, g, tokens].bitcast(E5M2),
                            lhsT_scale=x_scales[:, a, g, tokens],
                            rhs=w_codes["pass", c][:, g].bitcast(E4M3),
                            rhs_scale=w_scales["pass", c][:, g],
                            start=(g == 0),
                            stop=(g == PASSES - 1),
                        )
                banks.append((s0, acc))
            pass_bias = bias[:, PART * c : PART * (c + 1)].rearrange("p (h d) -> p h d", h=4)
            for s0, acc in banks:
                nc.vector.tensor_tensor(
                    out=results[u][:].rearrange("p h s d -> p s h d")[:, s0 : s0 + 2, :, ROT:P],
                    in0=acc[:].rearrange("p (s h d) -> p s h d", s=2, h=4),
                    in1=pass_bias.unsqueeze(1).to_broadcast([P, 2, 4, ROT]),
                    op=ADD,
                )

        def transpose_products(u):
            sums = ((products[u][0], products[u][2]), (products[u][3], products[u][1]))
            for s in range(TILES):
                if s % 2 == 0:
                    rotated[u, s] = bank("rot")
                for y, addends in enumerate(sums):
                    n0 = P * (2 * (s % 2) + y)
                    for i, product in enumerate(addends):
                        nc.tensor.matmul(
                            rotated[u, s - s % 2][:, n0 : n0 + P],
                            lhsT=product[:, P * s : P * (s + 1)],
                            rhs=ident_f32[:],
                            start=(i == 0),
                            stop=(i == 1),
                            is_transpose=True,
                        )

        def copy_rotated(u, s0):
            dst = results[u][:].rearrange("p h s d -> p s h d")[:, s0 : s0 + 2, :, 0:ROT]
            nc.scalar.copy(
                out=dst.rearrange("p s h (j y) -> p s h j y", y=2),
                in_=rotated[u, s0][:].rearrange("p (s y h j) -> p s h j y", s=2, y=2, j=PAIRS),
            )

        def store_queries(u, s0=0, s1=TILES):
            c, a = divmod(u, HALVES)
            store(results[u], out_0[0, 4 * c : 4 * (c + 1)], a, s0, s1)

        free_tags = ("rot", "rot", "pass", "pass")
        build_token_table()
        permute_bias()
        for s in range(TILES):
            transpose_x(0, s, free_tags[s])
        spread_bias()
        interleave_kv(0)
        nc.vector.tensor_scalar(out=neg_c1[:], in0=c1, scalar1=-1.0, scalar2=None, op0=MULT)
        quantize_w("kv", 0, 1)
        interleave_kv(1)
        quantize_x_half(0)
        quantize_w("kv", 1, 2)
        for s in range(TILES):
            transpose_x(1, s, free_tags[s])

        for s in range(TILES):
            multiply_kv(0, s, ("even", "odd")[s % 2])
        quantize_x_tiles(1, 0)
        interleave("rot", 0, 0)
        interleave("rot", 0, 1)
        add_kv_bias(0, 0)
        quantize_x_tiles(1, 2)
        for s in range(1, TILES):
            add_kv_bias(0, s)
        for s in range(TILES):
            multiply_kv(1, s, free_tags[s])
        quantize_w(("rot", 0))
        interleave("pass", 0, 0)
        interleave("pass", 0, 1)
        store(values[:, 0], out_2[0], 0)
        for s in range(TILES):
            add_kv_bias(1, s)
        quantize_w(("pass", 0))
        store(values[:, 1], out_2[0], 1)
        for a in range(HALVES):
            for s0 in range(0, TILES, 2):
                rotate_keys(a, s0)
        for a in range(HALVES):
            store(keys[:, a], out_1[0], a)

        pieces = [(part, c, g) for c in range(1, KV) for part in ("rot", "pass") for g in range(PASSES)]
        for piece in pieces[:LEAD]:
            interleave(*piece)
        multiply_rot(0)
        multiply_rot(1)
        form_products(0, 0, 4)

        last = UNITS - 1
        for u in range(last):
            part = ("rot", "pass")[u % HALVES]
            next_chunk = u // HALVES + 1
            round_pieces = pieces[LEAD + 2 * u : LEAD + 2 * u + 2]
            if round_pieces:
                interleave(*round_pieces[0])
            if u > 0:
                copy_rotated(u - 1, 0)
                copy_rotated(u - 1, 2)
                store_queries(u - 1)
            pass_channels(u)
            if round_pieces:
                interleave(*round_pieces[1])
            if u > 0:
                multiply_rot(u + 1)
            before = ROT_QUANTIZE_AFTER if part == "rot" else 0
            form_products(u + 1, 0, before)
            if next_chunk < KV:
                quantize_w((part, next_chunk))
            form_products(u + 1, before, 4)
            transpose_products(u)

        for s0 in range(0, TILES, 2):
            copy_rotated(last - 1, s0)
            store_queries(last - 1, s0, s0 + 2)
        pass_channels(last)
        transpose_products(last)
        for s0 in range(0, TILES, 2):
            copy_rotated(last, s0)
            store_queries(last, s0, s0 + 2)
